import numpy as np
import ml_dtypes


def mxq(x, axis, fmt="e4m3"):
    dtype, down = {"e4m3": (ml_dtypes.float8_e4m3fn, 7), "e5m2": (ml_dtypes.float8_e5m2, 14)}[fmt]
    v = np.moveaxis(np.asarray(x, np.float32).astype(ml_dtypes.bfloat16).astype(np.float64), axis, -1)
    blocks = v.reshape(v.shape[:-1] + (-1, 32))
    amax = np.abs(blocks).max(-1, keepdims=True)
    byte = np.maximum(np.where(amax > 0, np.frexp(amax)[1] - 1 + 127, 0) - down, 1)
    scale = np.exp2(byte - 127.0)
    codes = (blocks / scale).astype(np.float32).astype(dtype).astype(np.float64)
    return np.moveaxis((codes * scale).reshape(v.shape), -1, axis)


WIDE = False


def mx_kscale(k):
    if not WIDE:
        return np.ones(k)
    levels = np.array([18, -18])
    if k % 512:
        return np.exp2(np.random.permutation(np.resize(levels, k // 32))).repeat(32)
    a = np.empty((k // 512, 16))
    for p in range(k // 512):
        a[p, :8] = np.random.permutation(np.resize(levels, 8))
        for g in range(8):
            far = levels[np.abs(levels - a[p, g]) >= 10]
            a[p, g + 8] = far[np.random.randint(len(far))]
    return np.exp2(a.ravel()).repeat(32)


BF16 = ml_dtypes.bfloat16


def bf(x):
    return np.asarray(x, np.float32).astype(BF16)


def f64(x):
    return np.asarray(x).astype(np.float64)


T, D, H, C = 512, 1024, 8, 128
E = H * C
EPS = 1e-6
BASE = 10000.0


def rope_tables():
    inv_freq = 1.0 / BASE ** (np.arange(0, C, 2) / C)
    freqs = np.arange(T)[:, None] * inv_freq[None, :]
    return np.sin(freqs), np.cos(freqs)


def rotate_every_two(v):
    return np.stack((-v[..., 1::2], v[..., ::2]), axis=-1).reshape(v.shape)


def heads(v):
    return v.reshape(T, H, C).transpose(1, 0, 2)


def unheads(v):
    return v.transpose(1, 0, 2).reshape(T, E)


def project_and_stats(x, W_attn, b_attn):
    qk = f64(x) @ f64(W_attn)[:2 * E].T + f64(b_attn)[:2 * E]
    r = qk.reshape(T, 2 * H, C)
    return qk, r.mean(-1), 1.0 / np.sqrt(r.var(-1) + EPS)


def rope_backward(g, sin, cos):
    sin = np.repeat(sin, 2, axis=-1)[None]
    cos = np.repeat(cos, 2, axis=-1)[None]
    return g * cos - rotate_every_two(g) * sin


def norm_backward(g, w, v, mu, rs):
    vhat = (v - mu) * rs
    a = g * w
    return rs * (a - a.mean(-1, keepdims=True) - vhat * (a * vhat).mean(-1, keepdims=True))


def setup_inputs():
    s = mx_kscale(T)
    m = mx_kscale(3 * E)
    u = np.concatenate([np.repeat(m[:2 * E * 32 // C], C // 32), m[2 * E:]])
    ug = u.reshape(3, H, 1, C)
    x0 = bf(np.random.standard_normal((T, D)))
    W0 = bf(np.random.standard_normal((3 * E, D)) / np.sqrt(D))
    b_attn = bf(np.random.standard_normal(3 * E) * 0.3)
    q_ln_w = bf(1.0 + 0.2 * np.random.standard_normal(C))
    k_ln_w = bf(1.0 + 0.2 * np.random.standard_normal(C))
    g = []
    for i in range(3):
        n = np.random.standard_normal((H, T, C)) * np.exp2(np.random.randint(-6, 1, (1, T, 1)))
        g.append(bf(n / s[None, :, None] * ug[i]))
    qk, mean, rstd = project_and_stats(x0, W0, b_attn)
    return {"x": bf(f64(x0) * s[:, None]),
            "W_attn": bf(f64(W0) / u[:, None]),
            "b_attn": b_attn,
            "q_ln_w": q_ln_w,
            "k_ln_w": k_ln_w,
            "qk": np.asarray(qk, np.float32),
            "mean": np.asarray(mean, np.float32),
            "rstd": np.asarray(rstd, np.float32),
            "grad_0": g[0],
            "grad_1": g[1],
            "grad_2": g[2]}


def reference(x, W_attn, b_attn, q_ln_w, k_ln_w, qk, mean, rstd, grad_0, grad_1, grad_2):
    sin, cos = rope_tables()
    qkf = f64(qk)
    mu = f64(mean).T[:, :, None]
    rs = f64(rstd).T[:, :, None]
    dq = norm_backward(rope_backward(f64(grad_0), sin, cos), f64(q_ln_w), heads(qkf[:, :E]), mu[:H], rs[:H])
    dk = norm_backward(rope_backward(f64(grad_1), sin, cos), f64(k_ln_w), heads(qkf[:, E:]), mu[H:], rs[H:])
    dz = np.concatenate([unheads(dq), unheads(dk), unheads(f64(grad_2))], axis=1)
    dx = mxq(dz, 1, "e5m2") @ mxq(f64(W_attn), 0, "e4m3")
    dw = mxq(dz, 0, "e5m2").T @ mxq(f64(x), 0, "e4m3")
    return dx, dw

@@ -1,0 +1,480 @@
+import math
+from contextlib import ExitStack
+
+import concourse.mybir as mybir
+from concourse.masks import make_identity
+
+T, D, H, C = 512, 1024, 8, 128
+E = H * C
+P = 128
+FLOPS = 2 * 2 * T * 3 * E * D
+BYTES = (
+    T * D * 2 + 3 * E * D * 2 + 2 * C * 2 + T * 2 * E * 4 + 2 * T * 2 * H * 4
+    + 3 * H * T * C * 2 + T * D * 4 + 3 * E * D * 4
+)
+
+F32 = mybir.dt.float32
+BF16 = mybir.dt.bfloat16
+I32 = mybir.dt.int32
+U32 = mybir.dt.uint32
+U8 = mybir.dt.uint8
+E4 = mybir.dt.float8_e4m3fn_x4
+E5 = mybir.dt.float8_e5m2_x4
+ADD = mybir.AluOpType.add
+SUB = mybir.AluOpType.subtract
+MULT = mybir.AluOpType.mult
+ACT = mybir.ActivationFunctionType
+
+
+def tile_causalselfattention_pa_v_kernel(
+    tc, x, w_attn, b_attn, q_ln_w, k_ln_w, qk, mean, rstd, grad_0, grad_1, grad_2, out_0, out_1
+):
+    nc = tc.nc
+    with ExitStack() as ctx:
+        keep = ctx.enter_context(tc.tile_pool(name="keep", bufs=1))
+        load = ctx.enter_context(tc.tile_pool(name="load", bufs=2))
+        work = ctx.enter_context(tc.tile_pool(name="work", bufs=2))
+        psum = ctx.enter_context(tc.psum_pool(name="psum", bufs=8))
+        ctx.enter_context(tc.manual_schedule())
+
+        def load_g(grad, h0):
+            t = load.tile([P, 4, 512], BF16, name="g_raw", bufs=4)
+            nc.sync.dma_start(out=t[:], in_=grad[h0:h0 + 4].rearrange("h (p j) c -> p h (j c)", j=4))
+            return t
+
+        def load_u(n):
+            t = load.tile([P, 4, 512], F32, name="u_raw", bufs=3)
+            nc.sync.dma_start(out=t[:], in_=qk.rearrange("(p j) f -> p j f", j=4)[:, :, 512 * n:512 * n + 512])
+            return t
+
+        def load_w(src):
+            t = load.tile([P, 4, D], BF16, name="w_raw", bufs=3)
+            nc.sync.dma_start(out=t[:], in_=src.rearrange("(p j) d -> p j d", j=4))
+            return t
+
+        def w_rows(g):
+            return w_attn[512 * g:512 * g + 512, :]
+
+        gains_row = keep.tile([P, 2 * C], BF16)
+        nc.vector.memset(gains_row[:], 0.0)
+        mu = keep.tile([P, 4, 16], F32)
+        rs = keep.tile([P, 4, 16], F32)
+        nc.sync.dma_start(out=gains_row[0:1, 0:C], in_=q_ln_w.unsqueeze(0))
+        nc.sync.dma_start(out=gains_row[0:1, C:2 * C], in_=k_ln_w.unsqueeze(0))
+        v_raw = {4: load_g(grad_2, 0)}
+        nc.sync.dma_start(out=rs[:], in_=rstd.rearrange("(p j) n -> p j n", j=4))
+        nc.sync.dma_start(out=mu[:], in_=mean.rearrange("(p j) n -> p j n", j=4))
+        g_raw = {0: load_g(grad_0, 0)}
+        x_raw = load_w(x)
+        u_raw = {0: load_u(0)}
+        w_raw = {4: load_w(w_rows(4))}
+        g_raw[1] = load_g(grad_0, 4)
+        u_raw[1] = load_u(1)
+        w_raw[0] = load_w(w_rows(0))
+        v_raw[5] = load_g(grad_2, 4)
+
+        warm = keep.tile([P, 1], F32)
+        nc.gpsimd.memset(warm[:], 0.0)
+        nc.scalar.activation(out=warm[:], in_=warm[:], func=ACT.Sin)
+        tok = keep.tile([P, 4], F32)
+        nc.gpsimd.iota(tok[:], pattern=[[1, 4]], base=0, channel_multiplier=4, allow_small_or_imprecise_dtypes=True)
+        ident = keep.tile([P, P], F32)
+        make_identity(nc, ident[:])
+        ident_b = keep.tile([P, P], BF16)
+        nc.gpsimd.tensor_copy(out=ident_b[:], in_=ident[:])
+        ones = keep.tile([P, P], BF16)
+        nc.vector.memset(ones[:], 1.0)
+        turns = work.tile([P, 2, 4, 64], F32, name="turns", bufs=1)
+        nc.vector.tensor_scalar(out=turns[:, 0, :, 0:1], in0=tok[:].unsqueeze(2), scalar1=1.0 / (2.0 * math.pi), scalar2=None, op0=MULT)
+        for s in range(6):
+            n = 1 << s
+            nc.vector.tensor_scalar(out=turns[:, 0, :, n:2 * n], in0=turns[:, 0, :, 0:n], scalar1=10000.0 ** (-n / 64.0), scalar2=None, op0=MULT)
+        nc.vector.tensor_scalar(out=turns[:, 1], in0=turns[:, 0], scalar1=0.25, scalar2=None, op0=ADD)
+        whole = work.tile([P, 2, 4, 64], I32, name="whole", bufs=1)
+        nc.vector.tensor_copy(out=whole[:], in_=turns[:])
+        frac = work.tile([P, 2, 4, 64], F32, name="frac", bufs=1)
+        nc.vector.tensor_tensor(out=frac[:], in0=turns[:], in1=whole[:], op=SUB)
+        trig = keep.tile([P, 2, 4, 64], F32)
+        nc.scalar.activation(out=trig[:], in_=frac[:], func=ACT.Sin, scale=2.0 * math.pi)
+        gains_bank = psum.tile([P, 2 * C], F32, name="bank")
+        nc.tensor.matmul(gains_bank[:], lhsT=ones[:], rhs=gains_row[:], start=True, stop=True)
+        gains = keep.tile([P, 2, C], F32)
+        nc.scalar.copy(out=gains[:].rearrange("p w c -> p (w c)"), in_=gains_bank[:])
+
+        signed = keep.tile([P, 2, 64, 2], F32)
+        gv = gains[:].rearrange("p w (c e) -> p w c e", e=2)
+        nc.gpsimd.tensor_scalar(out=signed[:, :, :, 0:1], in0=gv[:, :, :, 0:1], scalar1=1.0, scalar2=0.0, op0=MULT, op1=ADD)
+        nc.gpsimd.tensor_scalar(out=signed[:, :, :, 1:2], in0=gv[:, :, :, 1:2], scalar1=-1.0, scalar2=0.0, op0=MULT, op1=ADD)
+        nmu = keep.tile([P, 4, 16], F32)
+        nc.gpsimd.tensor_scalar(out=nmu[:], in0=mu[:], scalar1=-1.0, scalar2=0.0, op0=MULT, op1=ADD)
+        r2 = keep.tile([P, 4, 16], F32)
+        nc.gpsimd.tensor_tensor(out=r2[:], in0=rs[:], in1=rs[:], op=MULT)
+        nc.gpsimd.tensor_scalar(out=r2[:], in0=r2[:], scalar1=-1.0 / C, scalar2=0.0, op0=MULT, op1=ADD)
+
+        ct = keep.tile([P, 2, 4, 64, 2], F32)
+        st = keep.tile([P, 2, 4, 64, 2], F32)
+
+        def tables(w):
+            nc.vector.tensor_tensor(out=ct[:, w], in0=trig[:, 1].unsqueeze(3).to_broadcast([P, 4, 64, 2]),
+                                    in1=gv[:, w].unsqueeze(1).to_broadcast([P, 4, 64, 2]), op=MULT)
+            nc.vector.tensor_tensor(out=st[:, w], in0=trig[:, 0].unsqueeze(3).to_broadcast([P, 4, 64, 2]),
+                                    in1=signed[:, w].unsqueeze(1).to_broadcast([P, 4, 64, 2]), op=MULT)
+
+        x_codes = keep.tile([P, D], U32, align_bytes=64)
+        x_scales = keep.tile([P, D], U8, align_bytes=64)
+        w_codes = keep.tile([P, 6, D], U32, align_bytes=64)
+        w_scales = keep.tile([P, 6, D], U8, align_bytes=64)
+        t_codes = keep.tile([P, 6, 512], U32, align_bytes=64)
+        t_scales = keep.tile([P, 6, 512], U8, align_bytes=64)
+
+        def copy(eng, dst, src):
+            if eng == "s":
+                nc.scalar.copy(out=dst, in_=src)
+            else:
+                nc.vector.tensor_copy(out=dst, in_=src)
+
+        def interleave(eng, dst, src):
+            copy(eng, dst.rearrange("p (c i) t -> p c t i", i=4), src.rearrange("p t (c i) -> p c t i", i=4))
+
+        def quant(codes, scales, src, fmt):
+            nc.vector.quantize_mx(out=codes.bitcast(fmt), scales=scales, in_=src.rearrange("p n t -> p (n t)"))
+
+        groups = {}
+
+        def new_group(g):
+            dz = work.tile([P, 512, 4], BF16, name="dz", align_bytes=64, bufs=2)
+            codes = work.tile([P, 512], U32, name="dzc", align_bytes=64, bufs=3)
+            scales = work.tile([P, 512], U8, name="dzs", align_bytes=64, bufs=3)
+            groups[g] = (dz, codes, scales)
+
+        ready = []
+
+        def mul_head(g, h):
+            codes, scales = groups[g][1], groups[g][2]
+            f = slice(128 * h, 128 * h + 128)
+            banks = []
+            for dh in range(2):
+                ps = psum.tile([P, 512], F32, name="bank")
+                d = slice(512 * dh, 512 * dh + 512)
+                nc.tensor.matmul_mx(out=ps[:], lhsT=codes[:, f].bitcast(E5), lhsT_scale=scales[:, f],
+                                    rhs=x_codes[:, d].bitcast(E4), rhs_scale=x_scales[:, d], start=True, stop=True)
+                banks.append(ps)
+            ready.append((512 * g + 128 * h, banks))
+
+        def drain_head(engs):
+            row0, banks = ready.pop(0)
+            o = work.tile([P, D], F32, name="o1", bufs=5)
+            for dh in range(2):
+                copy(engs[dh], o[:, 512 * dh:512 * dh + 512], banks[dh][:])
+            nc.sync.dma_start(out=out_1[row0:row0 + 128, :], in_=o[:])
+
+        turned = {}
+
+        def turn(g):
+            words = groups[g][0][:].rearrange("p f t -> p (f t)").bitcast(F32)
+            banks = []
+            for u in range(2):
+                tp = psum.tile([P, 4, P], F32, name="bank")
+                for t in range(4):
+                    nc.tensor.transpose(tp[:, t, :], words[:, 2 * t + u:1024:8], ident[:])
+                banks.append(tp)
+            turned[g] = banks
+
+        def untangle(g, engs):
+            dzt = work.tile([P, 512, 4], BF16, name="dzt", align_bytes=64, bufs=2)
+            for u in range(2):
+                copy(engs[u], dzt[:].rearrange("m (p u e) t -> m u p e t", u=2, e=2)[:, u],
+                     turned[g][u][:].rearrange("m t p -> m (t p)").bitcast(BF16).rearrange("m (t p e) -> m p e t", t=4, e=2))
+            turned[g] = dzt
+
+        def quant_turned(g):
+            quant(t_codes[:, g, :], t_scales[:, g, :], turned[g][:], E5)
+
+        w_order = [4, 0, 1, 5, 2, 3]
+        moved = {}
+        w_int = {}
+        w_wait = []
+
+        def w_move(k):
+            g, q = w_order[k // 4], k % 4
+            bank = psum.tile([P, 4, 256], BF16, name="bank")
+            for t in range(4):
+                nc.tensor.matmul(bank[:, t, :], lhsT=ident_b[:], rhs=w_raw[g][:, t, 256 * q:256 * q + 256], start=True, stop=True)
+            moved[k] = bank[:]
+
+        def w_spread(k, eng="s"):
+            g, q = w_order[k // 4], k % 4
+            if q % 2 == 0:
+                half = work.tile([P, 512, 4], BF16, name="w_int", align_bytes=64, bufs=3)
+                w_int[k // 2] = half
+            src = moved[k] if k in moved else w_raw[g][:, :, 256 * q:256 * q + 256]
+            interleave(eng, w_int[k // 2][:, 256 * (q % 2):256 * (q % 2) + 256, :], src)
+            if q % 2 == 1:
+                w_wait.append(k // 2)
+
+        def w_quant():
+            if w_wait:
+                m = w_wait.pop(0)
+                g, n0 = w_order[m // 2], 512 * (m % 2)
+                quant(w_codes[:, g, n0:n0 + 512], w_scales[:, g, n0:n0 + 512], w_int[m][:], E4)
+
+        units = [(2 * n, 2) for n in range(7)] + [(14, 1), (15, 1)]
+        state = [{} for n in range(len(units))]
+
+        def st_a(n):
+            i, m = units[n]
+            a = work.tile([P, 2, 512], F32, name="a", bufs=2)
+            tab = ct[:, i // 8].rearrange("p j c e -> p (j c e)").unsqueeze(1).to_broadcast([P, m, 512])
+            nc.vector.tensor_tensor(out=a[:, 0:m, :], in0=g_raw[i // 4][:, i % 4:i % 4 + m, :], in1=tab, op=MULT)
+            state[n]["a"] = a
+
+        def st_b(n):
+            i, m = units[n]
+            b = work.tile([P, 2, 512], F32, name="b", bufs=2)
+            for k in range(m):
+                for j in range(4):
+                    w = slice(128 * j, 128 * j + 128)
+                    nc.vector.scalar_tensor_tensor(
+                        out=b[:, k, w].rearrange("p (c e) -> p c e", e=2),
+                        in0=g_raw[i // 4][:, i % 4 + k, w].rearrange("p (c e) -> p c e", e=2)[:, :, ::-1],
+                        scalar=rs[:, j, i + k:i + k + 1], in1=st[:, i // 8, j], op0=MULT, op1=MULT)
+            state[n]["b"] = b
+
+        def st_c(n, by_scalar):
+            i, m = units[n]
+            a, b = state[n]["a"], state[n]["b"]
+            c = work.tile([P, 2, 512], F32, name="c", bufs=2)
+            q1 = work.tile([P, 2, 4], F32, name="q1", bufs=2)
+            for k in range(m):
+                for j in range(4):
+                    w = slice(128 * j, 128 * j + 128)
+                    nc.vector.scalar_tensor_tensor(
+                        out=c[:, k, w], in0=a[:, k, w], scalar=rs[:, j, i + k:i + k + 1], in1=b[:, k, w], op0=MULT, op1=ADD,
+                        accum_out=q1[:, k, j:j + 1])
+            state[n]["c"], state[n]["q1"] = c, q1
+
+        def st_q(n):
+            i, m = units[n]
+            a, c = state[n]["a"], state[n]["c"]
+            q2 = work.tile([P, 2, 4], F32, name="q2", bufs=2)
+            for k in range(m):
+                for j in range(4):
+                    w = slice(128 * j, 128 * j + 128)
+                    h = i % 4 + k
+                    nc.vector.scalar_tensor_tensor(
+                        out=a[:, k, w], in0=u_raw[i // 4][:, j, 128 * h:128 * h + 128], scalar=nmu[:, j, i + k:i + k + 1], in1=c[:, k, w],
+                        op0=ADD, op1=MULT, accum_out=q2[:, k, j:j + 1])
+            state[n]["q2"] = q2
+
+        def per_head(t, n):
+            i, m = units[n]
+            return t[:, :, i:i + m].rearrange("p j n -> p n j")
+
+        def st_k2(n):
+            i, m = units[n]
+            k2 = work.tile([P, 2, 4], F32, name="k2", bufs=2)
+            nc.vector.tensor_tensor(out=k2[:, 0:m], in0=state[n]["q2"][:, 0:m], in1=per_head(r2, n), op=MULT)
+            state[n]["k2"] = k2
+
+        def st_km(n):
+            i, m = units[n]
+            km = work.tile([P, 2, 4], F32, name="km", bufs=2)
+            nc.vector.tensor_tensor(out=km[:, 0:m], in0=state[n]["k2"][:, 0:m], in1=per_head(nmu, n), op=MULT)
+            state[n]["km"] = km
+
+        def st_k1(n):
+            i, m = units[n]
+            k1 = work.tile([P, 2, 4], F32, name="k1", bufs=2)
+            nc.vector.scalar_tensor_tensor(out=k1[:, 0:m], in0=state[n]["q1"][:, 0:m], scalar=-1.0 / C, in1=state[n]["km"][:, 0:m], op0=MULT, op1=ADD)
+            state[n]["k1"] = k1
+
+        def st_t(n):
+            i, m = units[n]
+            t1 = work.tile([P, 2, 512], F32, name="t1", bufs=2)
+            for k in range(m):
+                h = i % 4 + k
+                for j in range(4):
+                    nc.scalar.activation(out=t1[:, k, 128 * j:128 * j + 128], in_=u_raw[i // 4][:, j, 128 * h:128 * h + 128], func=ACT.Identity,
+                                         scale=state[n]["k2"][:, k, j:j + 1], bias=state[n]["k1"][:, k, j:j + 1])
+            state[n]["t1"] = t1
+
+        def st_f(n):
+            i, m = units[n]
+            if i % 4 == 0:
+                new_group(i // 4)
+            dz = groups[i // 4][0]
+            for k in range(m):
+                h = i % 4 + k
+                nc.vector.tensor_tensor(out=dz[:, 128 * h:128 * h + 128, :].rearrange("p (c i) t -> p c t i", i=4),
+                                        in0=state[n]["c"][:, k].rearrange("p (t c i) -> p c t i", t=4, i=4),
+                                        in1=state[n]["t1"][:, k].rearrange("p (t c i) -> p c t i", t=4, i=4), op=ADD)
+
+        def st_z(n):
+            i, m = units[n]
+            g = i // 4
+            dz, codes, scales = groups[g]
+            f = slice(128 * (i % 4), 128 * (i % 4 + m))
+            quant(codes[:, f], scales[:, f], dz[:, f, :], E5)
+            for k in range(m):
+                mul_head(g, i % 4 + k)
+
+        def out0_passes(ps, tb, dh, order, first, final):
+            t = slice(128 * tb, 128 * tb + 128)
+            d = slice(512 * dh, 512 * dh + 512)
+            for k, g in enumerate(order):
+                nc.tensor.matmul_mx(out=ps[:], lhsT=t_codes[:, g, t].bitcast(E5), lhsT_scale=t_scales[:, g, t],
+                                    rhs=w_codes[:, g, d].bitcast(E4), rhs_scale=w_scales[:, g, d],
+                                    start=first and k == 0, stop=final and k == len(order) - 1)
+
+        def v_interleave(g, h, eng):
+            interleave(eng, groups[g][0][:, 128 * h:128 * h + 128, :], v_raw[g][:, h, :].rearrange("p (t c) -> p t c", t=4))
+
+        new_group(4)
+        for h in range(4):
+            v_interleave(4, h, "v")
+        quant(groups[4][1][:], groups[4][2][:], groups[4][0][:], E5)
+        turn(4)
+        tables(0)
+        x_int = []
+        for q in range(4):
+            if q % 2 == 0:
+                half = work.tile([P, 512, 4], BF16, name="w_int", align_bytes=64, bufs=3)
+                x_int.append(half)
+            interleave("s", x_int[q // 2][:, 256 * (q % 2):256 * (q % 2) + 256, :], x_raw[:, :, 256 * q:256 * q + 256])
+        st_a(0)
+        st_b(0)
+        st_c(0, False)
+        untangle(4, "ss")
+        for q in range(2):
+            d = slice(512 * q, 512 * q + 512)
+            quant(x_codes[:, d], x_scales[:, d], x_int[q][:], E4)
+        for h in range(3):
+            mul_head(4, h)
+        st_q(0)
+        st_k2(0)
+        quant_turned(4)
+        st_km(0)
+        st_a(1)
+        st_k1(0)
+        for k in range(3):
+            drain_head("ss")
+        st_t(0)
+
+        next_w = 0
+        pieces = [0, 3, 4, 4, 4, 4, 4, 1, 0, 0]
+        direct = 6
+        to_untangle = []
+        to_quant = []
+        v1_next = 0
+
+        for n in range(1, 10):
+            last = n == 9
+            todo = list(range(next_w, next_w + pieces[n]))
+            next_w += pieces[n]
+            if n == 1:
+                w_raw[1] = load_w(w_rows(1))
+                g_raw[2] = load_g(grad_1, 0)
+                mul_head(4, 3)
+            if n == 2:
+                u_raw[2] = load_u(2)
+            if n == 3:
+                w_raw[5] = load_w(w_rows(5))
+                g_raw[3] = load_g(grad_1, 4)
+            if n == 4:
+                u_raw[3] = load_u(3)
+                w_raw[2] = load_w(w_rows(2))
+            if n == 5:
+                w_raw[3] = load_w(w_rows(3))
+            for k in todo[0:1]:
+                if k >= direct:
+                    w_move(k)
+            if to_untangle:
+                g = to_untangle.pop(0)
+                untangle(g, "ss")
+                to_quant.append(g)
+            for k in todo[0:1]:
+                w_spread(k)
+            if not last:
+                st_b(n)
+            for k in todo[1:3]:
+                if k >= direct:
+                    w_move(k)
+            while ready:
+                drain_head("ss")
+            if 5 <= n <= 8:
+                mul_head(5, n - 5)
+            if not last:
+                st_c(n, False)
+            for k in todo[1:3]:
+                w_spread(k)
+            while ready:
+                drain_head("ss")
+            if to_quant:
+                quant_turned(to_quant.pop(0))
+            st_f(n - 1)
+            for k in todo[3:]:
+                if k >= direct:
+                    w_move(k)
+            if not last:
+                st_q(n)
+            st_z(n - 1)
+            i, m = units[n - 1]
+            if (i + m) % 4 == 0:
+                turn((i + m) // 4 - 1)
+                to_untangle.append((i + m) // 4 - 1)
+            for k in todo[3:]:
+                w_spread(k)
+            if not last:
+                st_k2(n)
+                w_quant()
+                st_km(n)
+                if n < 8:
+                    st_a(n + 1)
+                st_k1(n)
+                w_quant()
+                st_t(n)
+            if n == 2:
+                tables(1)
+            if n in (3, 4):
+                if n == 3:
+                    new_group(5)
+                for h in (2 * n - 6, 2 * n - 5):
+                    v_interleave(5, h, "s")
+                if n == 4:
+                    quant(groups[5][1][:], groups[5][2][:], groups[5][0][:], E5)
+                    turn(5)
+                    to_untangle.append(5)
+            if n == 8:
+                while w_wait:
+                    w_quant()
+                parked = {}
+                for tb in (2, 3):
+                    for dh in range(2):
+                        ps = psum.tile([P, 512], F32, name="bank")
+                        out0_passes(ps, tb, dh, w_order[0:5], True, True)
+                        part = work.tile([P, 512], F32, name="part", bufs=4)
+                        nc.scalar.copy(out=part[:], in_=ps[:])
+                        parked[(tb, dh)] = part
+                opened = {}
+                for tb in (0, 1):
+                    for dh in range(2):
+                        ps = psum.tile([P, 512], F32, name="bank")
+                        out0_passes(ps, tb, dh, w_order[0:5], True, False)
+                        opened[(tb, dh)] = ps
+
+        untangle(3, "sv")
+        quant_turned(3)
+        while ready:
+            drain_head("sv")
+        for dh in range(2):
+            for tb in (2, 0, 3, 1):
+                o = work.tile([P, 512], F32, name="o0", bufs=4)
+                if tb < 2:
+                    ps = opened[(tb, dh)]
+                    out0_passes(ps, tb, dh, [3], False, True)
+                    nc.scalar.copy(out=o[:], in_=ps[:])
+                else:
+                    ps = psum.tile([P, 512], F32, name="bank")
+                    out0_passes(ps, tb, dh, [3], True, True)
+                    nc.vector.tensor_tensor(out=o[:], in0=ps[:], in1=parked[(tb, dh)][:], op=ADD)
+                nc.sync.dma_start(out=out_0[128 * tb:128 * tb + 128, 512 * dh:512 * dh + 512], in_=o[:])

@@ -84,15 +84,15 @@ def tile_causalselfattention_pa_v_kernel(
         nc.gpsimd.tensor_copy(out=ident_b[:], in_=ident[:])
         ones = keep.tile([P, P], BF16)
         nc.vector.memset(ones[:], 1.0)
-        turns = work.tile([P, 2, 4, 64], F32, name="turns", bufs=1)
+        turns = work.tile([P, 2, 4, 64], F32, name="part", bufs=4)
         nc.vector.tensor_scalar(out=turns[:, 0, :, 0:1], in0=tok[:].unsqueeze(2), scalar1=1.0 / (2.0 * math.pi), scalar2=None, op0=MULT)
         for s in range(6):
             n = 1 << s
             nc.vector.tensor_scalar(out=turns[:, 0, :, n:2 * n], in0=turns[:, 0, :, 0:n], scalar1=10000.0 ** (-n / 64.0), scalar2=None, op0=MULT)
         nc.vector.tensor_scalar(out=turns[:, 1], in0=turns[:, 0], scalar1=0.25, scalar2=None, op0=ADD)
-        whole = work.tile([P, 2, 4, 64], I32, name="whole", bufs=1)
+        whole = work.tile([P, 2, 4, 64], I32, name="part", bufs=4)
         nc.vector.tensor_copy(out=whole[:], in_=turns[:])
-        frac = work.tile([P, 2, 4, 64], F32, name="frac", bufs=1)
+        frac = work.tile([P, 2, 4, 64], F32, name="part", bufs=4)
         nc.vector.tensor_tensor(out=frac[:], in0=turns[:], in1=whole[:], op=SUB)
         trig = keep.tile([P, 2, 4, 64], F32)
         nc.scalar.activation(out=trig[:], in_=frac[:], func=ACT.Sin, scale=2.0 * math.pi)
@@ -163,7 +163,7 @@ def tile_causalselfattention_pa_v_kernel(
 
         def drain_head(engs):
             row0, banks = ready.pop(0)
-            o = work.tile([P, D], F32, name="o1", bufs=5)
+            o = work.tile([P, D], F32, name="o1", bufs=6)
             for dh in range(2):
                 copy(engs[dh], o[:, 512 * dh:512 * dh + 512], banks[dh][:])
             nc.sync.dma_start(out=out_1[row0:row0 + 128, :], in_=o[:])
@@ -190,7 +190,7 @@ def tile_causalselfattention_pa_v_kernel(
         def quant_turned(g):
             quant(t_codes[:, g, :], t_scales[:, g, :], turned[g][:], E5)
 
-        w_order = [4, 0, 1, 5, 2, 3]
+        w_order = [4, 0, 5, 1, 2, 3]
         moved = {}
         w_int = {}
         w_wait = []
@@ -220,6 +220,7 @@ def tile_causalselfattention_pa_v_kernel(
 
         units = [(2 * n, 2) for n in range(7)] + [(14, 1), (15, 1)]
         state = [{} for n in range(len(units))]
+        q1_by_scalar = ()
 
         def st_a(n):
             i, m = units[n]
@@ -240,7 +241,7 @@ def tile_causalselfattention_pa_v_kernel(
                         scalar=rs[:, j, i + k:i + k + 1], in1=st[:, i // 8, j], op0=MULT, op1=MULT)
             state[n]["b"] = b
 
-        def st_c(n, by_scalar):
+        def st_c(n):
             i, m = units[n]
             a, b = state[n]["a"], state[n]["b"]
             c = work.tile([P, 2, 512], F32, name="c", bufs=2)
@@ -250,7 +251,9 @@ def tile_causalselfattention_pa_v_kernel(
                     w = slice(128 * j, 128 * j + 128)
                     nc.vector.scalar_tensor_tensor(
                         out=c[:, k, w], in0=a[:, k, w], scalar=rs[:, j, i + k:i + k + 1], in1=b[:, k, w], op0=MULT, op1=ADD,
-                        accum_out=q1[:, k, j:j + 1])
+                        accum_out=None if n in q1_by_scalar else q1[:, k, j:j + 1])
+                    if n in q1_by_scalar:
+                        nc.scalar.activation(out=b[:, k, w], in_=c[:, k, w], func=ACT.Identity, accum_out=q1[:, k, j:j + 1])
             state[n]["c"], state[n]["q1"] = c, q1
 
         def st_q(n):
@@ -332,9 +335,9 @@ def tile_causalselfattention_pa_v_kernel(
         new_group(4)
         for h in range(4):
             v_interleave(4, h, "v")
+        tables(0)
         quant(groups[4][1][:], groups[4][2][:], groups[4][0][:], E5)
         turn(4)
-        tables(0)
         x_int = []
         for q in range(4):
             if q % 2 == 0:
@@ -343,7 +346,7 @@ def tile_causalselfattention_pa_v_kernel(
             interleave("s", x_int[q // 2][:, 256 * (q % 2):256 * (q % 2) + 256, :], x_raw[:, :, 256 * q:256 * q + 256])
         st_a(0)
         st_b(0)
-        st_c(0, False)
+        st_c(0)
         untangle(4, "ss")
         for q in range(2):
             d = slice(512 * q, 512 * q + 512)
@@ -356,125 +359,135 @@ def tile_causalselfattention_pa_v_kernel(
         st_km(0)
         st_a(1)
         st_k1(0)
-        for k in range(3):
-            drain_head("ss")
+        drain_head("ss")
         st_t(0)
+        while ready:
+            drain_head("ss")
 
         next_w = 0
-        pieces = [0, 3, 4, 4, 4, 4, 4, 1, 0, 0]
+        pieces = [0, 3, 4, 4, 4, 4, 4, 1, 0]
         direct = 6
         to_untangle = []
         to_quant = []
-        v1_next = 0
+        parked = {}
+        opened = {}
 
-        for n in range(1, 10):
-            last = n == 9
+        def open_bank(tb, dh):
+            ps = psum.tile([P, 512], F32, name="bank")
+            out0_passes(ps, tb, dh, w_order[0:5], True, False)
+            opened[(tb, dh)] = ps
+
+        def park_bank(tb, dh):
+            ps = psum.tile([P, 512], F32, name="bank")
+            out0_passes(ps, tb, dh, w_order[0:4], True, True)
+            part = work.tile([P, 512], F32, name="part", bufs=4)
+            nc.scalar.copy(out=part[:], in_=ps[:])
+            parked[(tb, dh)] = part
+
+        for n in range(1, 9):
             todo = list(range(next_w, next_w + pieces[n]))
             next_w += pieces[n]
             if n == 1:
-                w_raw[1] = load_w(w_rows(1))
+                w_raw[5] = load_w(w_rows(5))
                 g_raw[2] = load_g(grad_1, 0)
-                mul_head(4, 3)
             if n == 2:
                 u_raw[2] = load_u(2)
             if n == 3:
-                w_raw[5] = load_w(w_rows(5))
+                w_raw[1] = load_w(w_rows(1))
                 g_raw[3] = load_g(grad_1, 4)
             if n == 4:
                 u_raw[3] = load_u(3)
                 w_raw[2] = load_w(w_rows(2))
             if n == 5:
                 w_raw[3] = load_w(w_rows(3))
-            for k in todo[0:1]:
-                if k >= direct:
-                    w_move(k)
             if to_untangle:
                 g = to_untangle.pop(0)
                 untangle(g, "ss")
                 to_quant.append(g)
-            for k in todo[0:1]:
-                w_spread(k)
-            if not last:
-                st_b(n)
-            for k in todo[1:3]:
-                if k >= direct:
-                    w_move(k)
             while ready:
                 drain_head("ss")
-            if 5 <= n <= 8:
-                mul_head(5, n - 5)
-            if not last:
-                st_c(n, False)
-            for k in todo[1:3]:
+            for k in todo[0:2]:
+                if k >= direct:
+                    w_move(k)
+            for k in todo[0:2]:
                 w_spread(k)
+            st_b(n)
+            if n == 1:
+                mul_head(4, 3)
+            if n == 3:
+                quant(groups[5][1][:], groups[5][2][:], groups[5][0][:], E5)
+                turn(5)
+                to_untangle.append(5)
+            if 3 <= n <= 6:
+                mul_head(5, n - 3)
+            if n == 6:
+                park_bank(2, 0)
+                park_bank(2, 1)
+            if n == 8:
+                open_bank(1, 0)
+            st_c(n)
             while ready:
                 drain_head("ss")
             if to_quant:
                 quant_turned(to_quant.pop(0))
-            st_f(n - 1)
-            for k in todo[3:]:
+            if n == 7:
+                open_bank(0, 0)
+            for k in todo[2:]:
                 if k >= direct:
                     w_move(k)
-            if not last:
-                st_q(n)
+                    w_spread(k)
+            for k in todo[2:]:
+                if k < direct:
+                    w_spread(k)
+            if n == 6:
+                park_bank(3, 0)
+                park_bank(3, 1)
+            st_f(n - 1)
+            st_q(n)
             st_z(n - 1)
             i, m = units[n - 1]
             if (i + m) % 4 == 0:
                 turn((i + m) // 4 - 1)
                 to_untangle.append((i + m) // 4 - 1)
-            for k in todo[3:]:
-                w_spread(k)
-            if not last:
-                st_k2(n)
-                w_quant()
-                st_km(n)
-                if n < 8:
-                    st_a(n + 1)
-                st_k1(n)
-                w_quant()
-                st_t(n)
+            if n in (1, 2):
+                if n == 1:
+                    new_group(5)
+                for h in (2 * n - 2, 2 * n - 1):
+                    v_interleave(5, h, "s")
+            st_k2(n)
+            w_quant()
+            st_km(n)
+            if n < 8:
+                st_a(n + 1)
+            st_k1(n)
+            w_quant()
             if n == 2:
                 tables(1)
-            if n in (3, 4):
-                if n == 3:
-                    new_group(5)
-                for h in (2 * n - 6, 2 * n - 5):
-                    v_interleave(5, h, "s")
-                if n == 4:
-                    quant(groups[5][1][:], groups[5][2][:], groups[5][0][:], E5)
-                    turn(5)
-                    to_untangle.append(5)
+            st_t(n)
+            if n == 7:
+                open_bank(0, 1)
             if n == 8:
-                while w_wait:
-                    w_quant()
-                parked = {}
-                for tb in (2, 3):
-                    for dh in range(2):
-                        ps = psum.tile([P, 512], F32, name="bank")
-                        out0_passes(ps, tb, dh, w_order[0:5], True, True)
-                        part = work.tile([P, 512], F32, name="part", bufs=4)
-                        nc.scalar.copy(out=part[:], in_=ps[:])
-                        parked[(tb, dh)] = part
-                opened = {}
-                for tb in (0, 1):
-                    for dh in range(2):
-                        ps = psum.tile([P, 512], F32, name="bank")
-                        out0_passes(ps, tb, dh, w_order[0:5], True, False)
-                        opened[(tb, dh)] = ps
+                open_bank(1, 1)
 
+        while ready:
+            drain_head("ss")
+        st_f(8)
+        turn(3)
+        st_z(8)
         untangle(3, "sv")
         quant_turned(3)
         while ready:
             drain_head("sv")
-        for dh in range(2):
-            for tb in (2, 0, 3, 1):
-                o = work.tile([P, 512], F32, name="o0", bufs=4)
+        for k, tb in enumerate((0, 2, 1, 3)):
+            o = work.tile([P, D], F32, name="o1", bufs=6)
+            for dh in range(2):
+                d = slice(512 * dh, 512 * dh + 512)
                 if tb < 2:
                     ps = opened[(tb, dh)]
                     out0_passes(ps, tb, dh, [3], False, True)
-                    nc.scalar.copy(out=o[:], in_=ps[:])
+                    nc.scalar.copy(out=o[:, d], in_=ps[:])
                 else:
                     ps = psum.tile([P, 512], F32, name="bank")
-                    out0_passes(ps, tb, dh, [3], True, True)
-                    nc.vector.tensor_tensor(out=o[:], in0=ps[:], in1=parked[(tb, dh)][:], op=ADD)
-                nc.sync.dma_start(out=out_0[128 * tb:128 * tb + 128, 512 * dh:512 * dh + 512], in_=o[:])
+                    out0_passes(ps, tb, dh, [2, 3], True, True)
+                    nc.vector.tensor_tensor(out=o[:, d], in0=ps[:], in1=parked[(tb, dh)][:], op=ADD)
+                nc.sync.dma_start(out=out_0[128 * tb:128 * tb + 128, d], in_=o[:, d])

@@ -163,7 +163,7 @@ def tile_causalselfattention_pa_v_kernel(
 
         def drain_head(engs):
             row0, banks = ready.pop(0)
-            o = work.tile([P, D], F32, name="o1", bufs=6)
+            o = work.tile([P, D], F32, name="o1", bufs=5)
             for dh in range(2):
                 copy(engs[dh], o[:, 512 * dh:512 * dh + 512], banks[dh][:])
             nc.sync.dma_start(out=out_1[row0:row0 + 128, :], in_=o[:])
@@ -197,18 +197,23 @@ def tile_causalselfattention_pa_v_kernel(
 
         def w_move(k):
             g, q = w_order[k // 4], k % 4
-            bank = psum.tile([P, 4, 256], BF16, name="bank")
-            for t in range(4):
-                nc.tensor.matmul(bank[:, t, :], lhsT=ident_b[:], rhs=w_raw[g][:, t, 256 * q:256 * q + 256], start=True, stop=True)
+            bank = psum.tile([P, 256, 4], BF16, name="bank")
+            for t in (0, 2):
+                nc.tensor.matmul(bank[:, :, t:t + 2], lhsT=ident_b[:],
+                                 rhs=w_raw[g][:, t:t + 2, 256 * q:256 * q + 256].rearrange("p t c -> p c t"), start=True, stop=True)
             moved[k] = bank[:]
 
-        def w_spread(k, eng="s"):
+        def w_spread(k):
+            eng = "v" if k in by_vector else "s"
             g, q = w_order[k // 4], k % 4
             if q % 2 == 0:
-                half = work.tile([P, 512, 4], BF16, name="w_int", align_bytes=64, bufs=3)
+                half = work.tile([P, 512, 4], BF16, name="w_int", align_bytes=64, bufs=4)
                 w_int[k // 2] = half
-            src = moved[k] if k in moved else w_raw[g][:, :, 256 * q:256 * q + 256]
-            interleave(eng, w_int[k // 2][:, 256 * (q % 2):256 * (q % 2) + 256, :], src)
+            dst = w_int[k // 2][:, 256 * (q % 2):256 * (q % 2) + 256, :]
+            if k in moved:
+                copy(eng, dst, moved[k])
+            else:
+                interleave(eng, dst, w_raw[g][:, :, 256 * q:256 * q + 256])
             if q % 2 == 1:
                 w_wait.append(k // 2)
 
@@ -334,14 +339,14 @@ def tile_causalselfattention_pa_v_kernel(
 
         new_group(4)
         for h in range(4):
-            v_interleave(4, h, "v")
+            v_interleave(4, h, "vvss"[h])
         tables(0)
         quant(groups[4][1][:], groups[4][2][:], groups[4][0][:], E5)
         turn(4)
         x_int = []
         for q in range(4):
             if q % 2 == 0:
-                half = work.tile([P, 512, 4], BF16, name="w_int", align_bytes=64, bufs=3)
+                half = work.tile([P, 512, 4], BF16, name="w_int", align_bytes=64, bufs=4)
                 x_int.append(half)
             interleave("s", x_int[q // 2][:, 256 * (q % 2):256 * (q % 2) + 256, :], x_raw[:, :, 256 * q:256 * q + 256])
         st_a(0)
@@ -365,8 +370,9 @@ def tile_causalselfattention_pa_v_kernel(
             drain_head("ss")
 
         next_w = 0
-        pieces = [0, 3, 4, 4, 4, 4, 4, 1, 0]
-        direct = 6
+        pieces = [0, 3, 4, 4, 4, 4, 3, 2, 0]
+        direct = range(6)
+        by_vector = ()
         to_untangle = []
         to_quant = []
         parked = {}
@@ -407,7 +413,7 @@ def tile_causalselfattention_pa_v_kernel(
             while ready:
                 drain_head("ss")
             for k in todo[0:2]:
-                if k >= direct:
+                if k not in direct:
                     w_move(k)
             for k in todo[0:2]:
                 w_spread(k)
@@ -428,23 +434,23 @@ def tile_causalselfattention_pa_v_kernel(
             st_c(n)
             while ready:
                 drain_head("ss")
-            if to_quant:
-                quant_turned(to_quant.pop(0))
-            if n == 7:
-                open_bank(0, 0)
             for k in todo[2:]:
-                if k >= direct:
+                if k not in direct:
                     w_move(k)
                     w_spread(k)
             for k in todo[2:]:
-                if k < direct:
+                if k in direct:
                     w_spread(k)
             if n == 6:
                 park_bank(3, 0)
                 park_bank(3, 1)
             st_f(n - 1)
             st_q(n)
+            if to_quant:
+                quant_turned(to_quant.pop(0))
             st_z(n - 1)
+            if n == 7:
+                open_bank(0, 0)
             i, m = units[n - 1]
             if (i + m) % 4 == 0:
                 turn((i + m) // 4 - 1)
@@ -457,12 +463,16 @@ def tile_causalselfattention_pa_v_kernel(
             st_k2(n)
             w_quant()
             st_km(n)
+            if n == 8:
+                w_quant()
+                w_quant()
             if n < 8:
                 st_a(n + 1)
             st_k1(n)
-            w_quant()
             if n == 2:
                 tables(1)
+            if n in range(1, 6):
+                w_quant()
             st_t(n)
             if n == 7:
                 open_bank(0, 1)
@@ -471,6 +481,8 @@ def tile_causalselfattention_pa_v_kernel(
 
         while ready:
             drain_head("ss")
+        while w_wait:
+            w_quant()
         st_f(8)
         turn(3)
         st_z(8)
@@ -479,7 +491,7 @@ def tile_causalselfattention_pa_v_kernel(
         while ready:
             drain_head("sv")
         for k, tb in enumerate((0, 2, 1, 3)):
-            o = work.tile([P, D], F32, name="o1", bufs=6)
+            o = work.tile([P, D], F32, name="o1", bufs=5)
             for dh in range(2):
                 d = slice(512 * dh, 512 * dh + 512)
                 if tb < 2:

@@ -47,9 +47,18 @@ def tile_causalselfattention_pa_v_kernel(
             nc.sync.dma_start(out=t[:], in_=qk.rearrange("(p j) f -> p j f", j=4)[:, :, 512 * n:512 * n + 512])
             return t
 
-        def load_w(src):
+        def load_v(h0):
+            t = load.tile([P, 4, 512], BF16, name="g_raw", bufs=4)
+            for h in range(4):
+                nc.sync.dma_start(out=t[:, :, 128 * h:128 * h + 128], in_=grad_2[h0 + h].rearrange("(p j) c -> p j c", j=4))
+            return t
+
+        def load_w(src, parts=1):
             t = load.tile([P, 4, D], BF16, name="w_raw", bufs=3)
-            nc.sync.dma_start(out=t[:], in_=src.rearrange("(p j) d -> p j d", j=4))
+            rows = src.rearrange("(p j) d -> p j d", j=4)
+            n = D // parts
+            for k in range(parts):
+                nc.sync.dma_start(out=t[:, :, n * k:n * k + n], in_=rows[:, :, n * k:n * k + n])
             return t
 
         def w_rows(g):
@@ -61,23 +70,23 @@ def tile_causalselfattention_pa_v_kernel(
         rs = keep.tile([P, 4, 16], F32)
         nc.sync.dma_start(out=gains_row[0:1, 0:C], in_=q_ln_w.unsqueeze(0))
         nc.sync.dma_start(out=gains_row[0:1, C:2 * C], in_=k_ln_w.unsqueeze(0))
-        v_raw = {4: load_g(grad_2, 0)}
-        nc.sync.dma_start(out=rs[:], in_=rstd.rearrange("(p j) n -> p j n", j=4))
-        nc.sync.dma_start(out=mu[:], in_=mean.rearrange("(p j) n -> p j n", j=4))
         g_raw = {0: load_g(grad_0, 0)}
-        x_raw = load_w(x)
+        nc.sync.dma_start(out=rs[:], in_=rstd.rearrange("(p j) n -> p j n", j=4))
+        x_raw = load_w(x, 1)
         u_raw = {0: load_u(0)}
+        nc.sync.dma_start(out=mu[:], in_=mean.rearrange("(p j) n -> p j n", j=4))
         w_raw = {4: load_w(w_rows(4))}
+        v_raw = {4: load_v(0)}
         g_raw[1] = load_g(grad_0, 4)
         u_raw[1] = load_u(1)
         w_raw[0] = load_w(w_rows(0))
-        v_raw[5] = load_g(grad_2, 4)
+        v_raw[5] = load_v(4)
 
-        warm = keep.tile([P, 1], F32)
-        nc.gpsimd.memset(warm[:], 0.0)
-        nc.scalar.activation(out=warm[:], in_=warm[:], func=ACT.Sin)
         tok = keep.tile([P, 4], F32)
         nc.gpsimd.iota(tok[:], pattern=[[1, 4]], base=0, channel_multiplier=4, allow_small_or_imprecise_dtypes=True)
+        warm = keep.tile([P, 1], F32)
+        nc.vector.memset(warm[:], 0.0)
+        nc.scalar.activation(out=warm[:], in_=warm[:], func=ACT.Sin)
         ident = keep.tile([P, P], F32)
         make_identity(nc, ident[:])
         ident_b = keep.tile([P, P], BF16)
@@ -85,17 +94,21 @@ def tile_causalselfattention_pa_v_kernel(
         ones = keep.tile([P, P], BF16)
         nc.vector.memset(ones[:], 1.0)
         turns = work.tile([P, 2, 4, 64], F32, name="part", bufs=4)
-        nc.vector.tensor_scalar(out=turns[:, 0, :, 0:1], in0=tok[:].unsqueeze(2), scalar1=1.0 / (2.0 * math.pi), scalar2=None, op0=MULT)
-        for s in range(6):
-            n = 1 << s
-            nc.vector.tensor_scalar(out=turns[:, 0, :, n:2 * n], in0=turns[:, 0, :, 0:n], scalar1=10000.0 ** (-n / 64.0), scalar2=None, op0=MULT)
-        nc.vector.tensor_scalar(out=turns[:, 1], in0=turns[:, 0], scalar1=0.25, scalar2=None, op0=ADD)
         whole = work.tile([P, 2, 4, 64], I32, name="part", bufs=4)
-        nc.vector.tensor_copy(out=whole[:], in_=turns[:])
         frac = work.tile([P, 2, 4, 64], F32, name="part", bufs=4)
-        nc.vector.tensor_tensor(out=frac[:], in0=turns[:], in1=whole[:], op=SUB)
         trig = keep.tile([P, 2, 4, 64], F32)
-        nc.scalar.activation(out=trig[:], in_=frac[:], func=ACT.Sin, scale=2.0 * math.pi)
+        nc.vector.tensor_scalar(out=turns[:, 0, :, 0:1], in0=tok[:].unsqueeze(2), scalar1=1.0 / (2.0 * math.pi), scalar2=None, op0=MULT)
+        for n in (1, 4, 16):
+            for k in (1, 2, 3):
+                nc.vector.tensor_scalar(out=turns[:, 0, :, n * k:n * k + n], in0=turns[:, 0, :, 0:n],
+                                        scalar1=10000.0 ** (-n * k / 64.0), scalar2=None, op0=MULT)
+        for k in (1, 0):
+            if k == 1:
+                nc.vector.tensor_scalar(out=turns[:, 1], in0=turns[:, 0], scalar1=0.25, scalar2=None, op0=ADD)
+            nc.vector.tensor_copy(out=whole[:, k], in_=turns[:, k])
+        for k in (1, 0):
+            nc.vector.tensor_tensor(out=frac[:, k], in0=turns[:, k], in1=whole[:, k], op=SUB)
+            nc.scalar.activation(out=trig[:, k], in_=frac[:, k], func=ACT.Sin, scale=2.0 * math.pi)
         gains_bank = psum.tile([P, 2 * C], F32, name="bank")
         nc.tensor.matmul(gains_bank[:], lhsT=ones[:], rhs=gains_row[:], start=True, stop=True)
         gains = keep.tile([P, 2, C], F32)
@@ -114,9 +127,11 @@ def tile_causalselfattention_pa_v_kernel(
         ct = keep.tile([P, 2, 4, 64, 2], F32)
         st = keep.tile([P, 2, 4, 64, 2], F32)
 
-        def tables(w):
+        def cos_table(w, source):
             nc.vector.tensor_tensor(out=ct[:, w], in0=trig[:, 1].unsqueeze(3).to_broadcast([P, 4, 64, 2]),
-                                    in1=gv[:, w].unsqueeze(1).to_broadcast([P, 4, 64, 2]), op=MULT)
+                                    in1=source.rearrange("p (c e) -> p c e", e=2).unsqueeze(1).to_broadcast([P, 4, 64, 2]), op=MULT)
+
+        def sin_table(w):
             nc.vector.tensor_tensor(out=st[:, w], in0=trig[:, 0].unsqueeze(3).to_broadcast([P, 4, 64, 2]),
                                     in1=signed[:, w].unsqueeze(1).to_broadcast([P, 4, 64, 2]), op=MULT)
 
@@ -143,8 +158,8 @@ def tile_causalselfattention_pa_v_kernel(
 
         def new_group(g):
             dz = work.tile([P, 512, 4], BF16, name="dz", align_bytes=64, bufs=2)
-            codes = work.tile([P, 512], U32, name="dzc", align_bytes=64, bufs=3)
-            scales = work.tile([P, 512], U8, name="dzs", align_bytes=64, bufs=3)
+            codes = work.tile([P, 512], U32, name="dzc", align_bytes=64, bufs=4)
+            scales = work.tile([P, 512], U8, name="dzs", align_bytes=64, bufs=4)
             groups[g] = (dz, codes, scales)
 
         ready = []
@@ -180,7 +195,28 @@ def tile_causalselfattention_pa_v_kernel(
                 banks.append(tp)
             turned[g] = banks
 
+        def turn_v(g):
+            banks = []
+            for b in range(2):
+                tp = psum.tile([P, 2, 2, P], F32, name="bank")
+                for k in range(2):
+                    words = v_raw[g][:, 2 * b + k, :].bitcast(F32)
+                    for u in range(2):
+                        nc.tensor.transpose(tp[:, k, u, :], words[:, u:256:2], ident[:])
+                banks.append(tp)
+            turned[g] = banks
+
+        def untangle_v(g, engs):
+            dzt = work.tile([P, 512, 4], BF16, name="dzt", align_bytes=64, bufs=2)
+            words = dzt[:].rearrange("m n t -> m (n t)").bitcast(F32).rearrange("m (p b k) -> m b p k", b=2, k=4)
+            for b in range(2):
+                copy(engs[b], words[:, b], turned[g][b][:].rearrange("m k u p -> m p (k u)"))
+            turned[g] = dzt
+
         def untangle(g, engs):
+            if g >= 4:
+                untangle_v(g, engs)
+                return
             dzt = work.tile([P, 512, 4], BF16, name="dzt", align_bytes=64, bufs=2)
             for u in range(2):
                 copy(engs[u], dzt[:].rearrange("m (p u e) t -> m u p e t", u=2, e=2)[:, u],
@@ -302,8 +338,12 @@ def tile_causalselfattention_pa_v_kernel(
             for k in range(m):
                 h = i % 4 + k
                 for j in range(4):
-                    nc.scalar.activation(out=t1[:, k, 128 * j:128 * j + 128], in_=u_raw[i // 4][:, j, 128 * h:128 * h + 128], func=ACT.Identity,
-                                         scale=state[n]["k2"][:, k, j:j + 1], bias=state[n]["k1"][:, k, j:j + 1])
+                    o, u = t1[:, k, 128 * j:128 * j + 128], u_raw[i // 4][:, j, 128 * h:128 * h + 128]
+                    k2, k1 = state[n]["k2"][:, k, j:j + 1], state[n]["k1"][:, k, j:j + 1]
+                    if n == 8 and j >= 1:
+                        nc.vector.tensor_scalar(out=o, in0=u, scalar1=k2, scalar2=k1, op0=MULT, op1=ADD)
+                    else:
+                        nc.scalar.activation(out=o, in_=u, func=ACT.Identity, scale=k2, bias=k1)
             state[n]["t1"] = t1
 
         def st_f(n):
@@ -335,14 +375,11 @@ def tile_causalselfattention_pa_v_kernel(
                                     start=first and k == 0, stop=final and k == len(order) - 1)
 
         def v_interleave(g, h, eng):
-            interleave(eng, groups[g][0][:, 128 * h:128 * h + 128, :], v_raw[g][:, h, :].rearrange("p (t c) -> p t c", t=4))
+            interleave(eng, groups[g][0][:, 128 * h:128 * h + 128, :], v_raw[g][:, :, 128 * h:128 * h + 128])
 
-        new_group(4)
-        for h in range(4):
-            v_interleave(4, h, "vvss"[h])
-        tables(0)
-        quant(groups[4][1][:], groups[4][2][:], groups[4][0][:], E5)
-        turn(4)
+        direct = (0, 1, 2, 4, 8, 12)
+        by_vector = ()
+        cos_table(0, gains_bank[:, 0:C])
         x_int = []
         for q in range(4):
             if q % 2 == 0:
@@ -350,30 +387,29 @@ def tile_causalselfattention_pa_v_kernel(
                 x_int.append(half)
             interleave("s", x_int[q // 2][:, 256 * (q % 2):256 * (q % 2) + 256, :], x_raw[:, :, 256 * q:256 * q + 256])
         st_a(0)
+        sin_table(0)
         st_b(0)
         st_c(0)
-        untangle(4, "ss")
+        new_group(4)
+        for k in range(1):
+            w_spread(k)
+        for h in range(4):
+            v_interleave(4, h, "s")
+        st_q(0)
+        st_k2(0)
         for q in range(2):
             d = slice(512 * q, 512 * q + 512)
             quant(x_codes[:, d], x_scales[:, d], x_int[q][:], E4)
-        for h in range(3):
-            mul_head(4, h)
-        st_q(0)
-        st_k2(0)
-        quant_turned(4)
-        st_km(0)
-        st_a(1)
+            if q == 0:
+                st_km(0)
         st_k1(0)
-        drain_head("ss")
+        turn_v(4)
+        st_a(1)
         st_t(0)
-        while ready:
-            drain_head("ss")
 
-        next_w = 0
-        pieces = [0, 3, 4, 4, 4, 4, 3, 2, 0]
-        direct = range(6)
-        by_vector = ()
-        to_untangle = []
+        next_w = len(range(1))
+        pieces = [0, 3, 4, 4, 4, 4, 2, 2, 0]
+        to_untangle = [4]
         to_quant = []
         parked = {}
         opened = {}
@@ -419,13 +455,17 @@ def tile_causalselfattention_pa_v_kernel(
                 w_spread(k)
             st_b(n)
             if n == 1:
+                quant(groups[4][1][:], groups[4][2][:], groups[4][0][:], E5)
+                for h in range(3):
+                    mul_head(4, h)
+            if n == 2:
                 mul_head(4, 3)
             if n == 3:
                 quant(groups[5][1][:], groups[5][2][:], groups[5][0][:], E5)
-                turn(5)
+                turn_v(5)
                 to_untangle.append(5)
-            if 3 <= n <= 6:
-                mul_head(5, n - 3)
+            for h in {3: (0,), 4: (1,), 5: (2,), 6: (3,)}.get(n, ()):
+                mul_head(5, h)
             if n == 6:
                 park_bank(2, 0)
                 park_bank(2, 1)
@@ -446,11 +486,7 @@ def tile_causalselfattention_pa_v_kernel(
                 park_bank(3, 1)
             st_f(n - 1)
             st_q(n)
-            if to_quant:
-                quant_turned(to_quant.pop(0))
             st_z(n - 1)
-            if n == 7:
-                open_bank(0, 0)
             i, m = units[n - 1]
             if (i + m) % 4 == 0:
                 turn((i + m) // 4 - 1)
@@ -461,7 +497,12 @@ def tile_causalselfattention_pa_v_kernel(
                 for h in (2 * n - 2, 2 * n - 1):
                     v_interleave(5, h, "s")
             st_k2(n)
-            w_quant()
+            if to_quant:
+                quant_turned(to_quant.pop(0))
+            if n == 7:
+                open_bank(0, 0)
+            if n in range(1, 7):
+                w_quant()
             st_km(n)
             if n == 8:
                 w_quant()
@@ -470,8 +511,9 @@ def tile_causalselfattention_pa_v_kernel(
                 st_a(n + 1)
             st_k1(n)
             if n == 2:
-                tables(1)
-            if n in range(1, 6):
+                cos_table(1, gains[:, 1])
+                sin_table(1)
+            if n in range(2, 6):
                 w_quant()
             st_t(n)
             if n == 7:
@@ -481,11 +523,15 @@ def tile_causalselfattention_pa_v_kernel(
 
         while ready:
             drain_head("ss")
+        for h in ():
+            mul_head(5, h)
         while w_wait:
             w_quant()
         st_f(8)
         turn(3)
         st_z(8)
+        for h in ():
+            drain_head("sv")
         untangle(3, "sv")
         quant_turned(3)
         while ready:

@@ -84,6 +84,10 @@ def tile_causalselfattention_pa_v_kernel(
 
         tok = keep.tile([P, 4], F32)
         nc.gpsimd.iota(tok[:], pattern=[[1, 4]], base=0, channel_multiplier=4, allow_small_or_imprecise_dtypes=True)
+        channel = keep.tile([P, 1], I32)
+        nc.gpsimd.iota(channel[:], pattern=[[0, 1]], base=0, channel_multiplier=1)
+        sign = keep.tile([P, 1], F32)
+        odd = keep.tile([P, 1], I32)
         warm = keep.tile([P, 1], F32)
         nc.vector.memset(warm[:], 0.0)
         nc.scalar.activation(out=warm[:], in_=warm[:], func=ACT.Sin)
@@ -96,44 +100,58 @@ def tile_causalselfattention_pa_v_kernel(
         turns = work.tile([P, 2, 4, 64], F32, name="part", bufs=4)
         whole = work.tile([P, 2, 4, 64], I32, name="part", bufs=4)
         frac = work.tile([P, 2, 4, 64], F32, name="part", bufs=4)
-        trig = keep.tile([P, 2, 4, 64], F32)
+        nc.vector.tensor_scalar(out=odd[:], in0=channel[:], scalar1=1, scalar2=None, op0=mybir.AluOpType.bitwise_and)
         nc.vector.tensor_scalar(out=turns[:, 0, :, 0:1], in0=tok[:].unsqueeze(2), scalar1=1.0 / (2.0 * math.pi), scalar2=None, op0=MULT)
         for n in (1, 4, 16):
             for k in (1, 2, 3):
                 nc.vector.tensor_scalar(out=turns[:, 0, :, n * k:n * k + n], in0=turns[:, 0, :, 0:n],
                                         scalar1=10000.0 ** (-n * k / 64.0), scalar2=None, op0=MULT)
+        nc.vector.tensor_scalar(out=sign[:], in0=odd[:], scalar1=-2.0, scalar2=1.0, op0=MULT, op1=ADD)
         for k in (1, 0):
             if k == 1:
                 nc.vector.tensor_scalar(out=turns[:, 1], in0=turns[:, 0], scalar1=0.25, scalar2=None, op0=ADD)
             nc.vector.tensor_copy(out=whole[:, k], in_=turns[:, k])
         for k in (1, 0):
             nc.vector.tensor_tensor(out=frac[:, k], in0=turns[:, k], in1=whole[:, k], op=SUB)
-            nc.scalar.activation(out=trig[:, k], in_=frac[:, k], func=ACT.Sin, scale=2.0 * math.pi)
+        sines = work.tile([P, 4, 64, 2], F32, name="part", bufs=4)
+        cosines = keep.tile([P, 4, 64], F32)
+        nc.scalar.activation(out=cosines[:], in_=frac[:, 1], func=ACT.Sin, scale=2.0 * math.pi)
+        nc.scalar.activation(out=sines[:], in_=frac[:, 0].unsqueeze(3).to_broadcast([P, 4, 64, 2]), func=ACT.Sin, scale=2.0 * math.pi)
         gains_bank = psum.tile([P, 2 * C], F32, name="bank")
         nc.tensor.matmul(gains_bank[:], lhsT=ones[:], rhs=gains_row[:], start=True, stop=True)
         gains = keep.tile([P, 2, C], F32)
         nc.scalar.copy(out=gains[:].rearrange("p w c -> p (w c)"), in_=gains_bank[:])
+        column_bank = psum.tile([P, 2, 2], F32, name="bank")
+        for w in range(2):
+            nc.tensor.matmul(column_bank[:, w, :], lhsT=gains_row[:, C * w:C * w + C], rhs=ones[:, 0:2], start=True, stop=True)
+        sines_bank = psum.tile([P, 4, P], F32, name="bank")
+        for j in range(4):
+            nc.tensor.transpose(sines_bank[:, j, :], sines[:, j].rearrange("p c e -> p (c e)"), ident[:])
+        column = keep.tile([P, 2], F32)
+        nc.vector.tensor_scalar(out=column[:], in0=column_bank[:, :, 0], scalar1=sign[:], scalar2=None, op0=MULT)
+        sines_by_channel = []
+        for w in range(2):
+            t = keep.tile([P, 4, P], F32, name="sines_t%d" % w)
+            nc.scalar.activation(out=t[:], in_=sines_bank[:], func=ACT.Copy, scale=column[:, w:w + 1])
+            sines_by_channel.append(t)
 
-        signed = keep.tile([P, 2, 64, 2], F32)
-        gv = gains[:].rearrange("p w (c e) -> p w c e", e=2)
-        nc.gpsimd.tensor_scalar(out=signed[:, :, :, 0:1], in0=gv[:, :, :, 0:1], scalar1=1.0, scalar2=0.0, op0=MULT, op1=ADD)
-        nc.gpsimd.tensor_scalar(out=signed[:, :, :, 1:2], in0=gv[:, :, :, 1:2], scalar1=-1.0, scalar2=0.0, op0=MULT, op1=ADD)
         nmu = keep.tile([P, 4, 16], F32)
-        nc.gpsimd.tensor_scalar(out=nmu[:], in0=mu[:], scalar1=-1.0, scalar2=0.0, op0=MULT, op1=ADD)
         r2 = keep.tile([P, 4, 16], F32)
         nc.gpsimd.tensor_tensor(out=r2[:], in0=rs[:], in1=rs[:], op=MULT)
         nc.gpsimd.tensor_scalar(out=r2[:], in0=r2[:], scalar1=-1.0 / C, scalar2=0.0, op0=MULT, op1=ADD)
 
         ct = keep.tile([P, 2, 4, 64, 2], F32)
-        st = keep.tile([P, 2, 4, 64, 2], F32)
+        st = {}
 
         def cos_table(w, source):
-            nc.vector.tensor_tensor(out=ct[:, w], in0=trig[:, 1].unsqueeze(3).to_broadcast([P, 4, 64, 2]),
+            nc.vector.tensor_tensor(out=ct[:, w], in0=cosines[:].unsqueeze(3).to_broadcast([P, 4, 64, 2]),
                                     in1=source.rearrange("p (c e) -> p c e", e=2).unsqueeze(1).to_broadcast([P, 4, 64, 2]), op=MULT)
 
         def sin_table(w):
-            nc.vector.tensor_tensor(out=st[:, w], in0=trig[:, 0].unsqueeze(3).to_broadcast([P, 4, 64, 2]),
-                                    in1=signed[:, w].unsqueeze(1).to_broadcast([P, 4, 64, 2]), op=MULT)
+            bank = psum.tile([P, 4, P], F32, name="bank")
+            for j in range(4):
+                nc.tensor.transpose(bank[:, j, :], sines_by_channel[w][:, j, :], ident[:])
+            st[w] = bank
 
         x_codes = keep.tile([P, D], U32, align_bytes=64)
         x_scales = keep.tile([P, D], U8, align_bytes=64)
@@ -263,12 +281,28 @@ def tile_causalselfattention_pa_v_kernel(
         state = [{} for n in range(len(units))]
         q1_by_scalar = ()
 
+        def table(n, cols):
+            return ct[:, units[n][0] // 8].rearrange("p j c e -> p (j c e)")[:, cols]
+
+        def by_gpsimd(n):
+            return 384 if 1 <= n <= 6 else 0
+
+        def st_ag(n):
+            i, m = units[n]
+            a1 = work.tile([P, 512], F32, name="a1", bufs=1)
+            g = by_gpsimd(n)
+            if g:
+                nc.gpsimd.tensor_tensor(out=a1[:, 0:g], in0=g_raw[i // 4][:, i % 4 + 1, 0:g], in1=table(n, slice(0, g)), op=MULT)
+            state[n]["a1"] = a1
+
         def st_a(n):
             i, m = units[n]
-            a = work.tile([P, 2, 512], F32, name="a", bufs=2)
-            tab = ct[:, i // 8].rearrange("p j c e -> p (j c e)").unsqueeze(1).to_broadcast([P, m, 512])
-            nc.vector.tensor_tensor(out=a[:, 0:m, :], in0=g_raw[i // 4][:, i % 4:i % 4 + m, :], in1=tab, op=MULT)
-            state[n]["a"] = a
+            a0 = work.tile([P, 512], F32, name="a0", bufs=2)
+            nc.vector.tensor_tensor(out=a0[:], in0=g_raw[i // 4][:, i % 4, :], in1=table(n, slice(0, 512)), op=MULT)
+            g = by_gpsimd(n)
+            if m == 2 and g < 512:
+                nc.vector.tensor_tensor(out=state[n]["a1"][:, g:512], in0=g_raw[i // 4][:, i % 4 + 1, g:512], in1=table(n, slice(g, 512)), op=MULT)
+            state[n]["a0"] = a0
 
         def st_b(n):
             i, m = units[n]
@@ -279,19 +313,19 @@ def tile_causalselfattention_pa_v_kernel(
                     nc.vector.scalar_tensor_tensor(
                         out=b[:, k, w].rearrange("p (c e) -> p c e", e=2),
                         in0=g_raw[i // 4][:, i % 4 + k, w].rearrange("p (c e) -> p c e", e=2)[:, :, ::-1],
-                        scalar=rs[:, j, i + k:i + k + 1], in1=st[:, i // 8, j], op0=MULT, op1=MULT)
+                        scalar=rs[:, j, i + k:i + k + 1], in1=st[i // 8][:, j, :].rearrange("p (c e) -> p c e", e=2), op0=MULT, op1=MULT)
             state[n]["b"] = b
 
         def st_c(n):
             i, m = units[n]
-            a, b = state[n]["a"], state[n]["b"]
+            a, b = (state[n]["a0"], state[n]["a1"]), state[n]["b"]
             c = work.tile([P, 2, 512], F32, name="c", bufs=2)
             q1 = work.tile([P, 2, 4], F32, name="q1", bufs=2)
             for k in range(m):
                 for j in range(4):
                     w = slice(128 * j, 128 * j + 128)
                     nc.vector.scalar_tensor_tensor(
-                        out=c[:, k, w], in0=a[:, k, w], scalar=rs[:, j, i + k:i + k + 1], in1=b[:, k, w], op0=MULT, op1=ADD,
+                        out=c[:, k, w], in0=a[k][:, w], scalar=rs[:, j, i + k:i + k + 1], in1=b[:, k, w], op0=MULT, op1=ADD,
                         accum_out=None if n in q1_by_scalar else q1[:, k, j:j + 1])
                     if n in q1_by_scalar:
                         nc.scalar.activation(out=b[:, k, w], in_=c[:, k, w], func=ACT.Identity, accum_out=q1[:, k, j:j + 1])
@@ -299,14 +333,16 @@ def tile_causalselfattention_pa_v_kernel(
 
         def st_q(n):
             i, m = units[n]
-            a, c = state[n]["a"], state[n]["c"]
+            a, c = (state[n]["a0"], state[n]["a1"]), state[n]["c"]
             q2 = work.tile([P, 2, 4], F32, name="q2", bufs=2)
-            for k in range(m):
-                for j in range(4):
+            rows = [(0, j) for j in range(4)]
+            if m == 2:
+                rows = rows[0:3] + [(1, j) for j in range(4)] + rows[3:]
+            for k, j in rows:
                     w = slice(128 * j, 128 * j + 128)
                     h = i % 4 + k
                     nc.vector.scalar_tensor_tensor(
-                        out=a[:, k, w], in0=u_raw[i // 4][:, j, 128 * h:128 * h + 128], scalar=nmu[:, j, i + k:i + k + 1], in1=c[:, k, w],
+                        out=a[k][:, w], in0=u_raw[i // 4][:, j, 128 * h:128 * h + 128], scalar=nmu[:, j, i + k:i + k + 1], in1=c[:, k, w],
                         op0=ADD, op1=MULT, accum_out=q2[:, k, j:j + 1])
             state[n]["q2"] = q2
 
@@ -340,7 +376,7 @@ def tile_causalselfattention_pa_v_kernel(
                 for j in range(4):
                     o, u = t1[:, k, 128 * j:128 * j + 128], u_raw[i // 4][:, j, 128 * h:128 * h + 128]
                     k2, k1 = state[n]["k2"][:, k, j:j + 1], state[n]["k1"][:, k, j:j + 1]
-                    if n == 8 and j >= 1:
+                    if n >= 6 and 4 * k + j >= (4, 0, 1)[n - 6]:
                         nc.vector.tensor_scalar(out=o, in0=u, scalar1=k2, scalar2=k1, op0=MULT, op1=ADD)
                     else:
                         nc.scalar.activation(out=o, in_=u, func=ACT.Identity, scale=k2, bias=k1)
@@ -378,7 +414,7 @@ def tile_causalselfattention_pa_v_kernel(
             interleave(eng, groups[g][0][:, 128 * h:128 * h + 128, :], v_raw[g][:, :, 128 * h:128 * h + 128])
 
         direct = (0, 1, 2, 4, 8, 12)
-        by_vector = ()
+        by_vector = (1,)
         cos_table(0, gains_bank[:, 0:C])
         x_int = []
         for q in range(4):
@@ -386,16 +422,20 @@ def tile_causalselfattention_pa_v_kernel(
                 half = work.tile([P, 512, 4], BF16, name="w_int", align_bytes=64, bufs=4)
                 x_int.append(half)
             interleave("s", x_int[q // 2][:, 256 * (q % 2):256 * (q % 2) + 256, :], x_raw[:, :, 256 * q:256 * q + 256])
-        st_a(0)
         sin_table(0)
+        st_ag(0)
+        st_a(0)
         st_b(0)
         st_c(0)
+        nc.vector.tensor_scalar(out=nmu[:], in0=mu[:], scalar1=-1.0, scalar2=None, op0=MULT)
         new_group(4)
         for k in range(1):
             w_spread(k)
         for h in range(4):
             v_interleave(4, h, "s")
         st_q(0)
+        st_ag(1)
+        st_b(1)
         st_k2(0)
         for q in range(2):
             d = slice(512 * q, 512 * q + 512)
@@ -453,7 +493,6 @@ def tile_causalselfattention_pa_v_kernel(
                     w_move(k)
             for k in todo[0:2]:
                 w_spread(k)
-            st_b(n)
             if n == 1:
                 quant(groups[4][1][:], groups[4][2][:], groups[4][0][:], E5)
                 for h in range(3):
@@ -486,6 +525,9 @@ def tile_causalselfattention_pa_v_kernel(
                 park_bank(3, 1)
             st_f(n - 1)
             st_q(n)
+            if n < 8:
+                st_ag(n + 1)
+                st_b(n + 1)
             st_z(n - 1)
             i, m = units[n - 1]
             if (i + m) % 4 == 0:

import math
from contextlib import ExitStack

import concourse.mybir as mybir
from concourse.masks import make_identity

T, D, H, C = 512, 1024, 8, 128
E = H * C
P = 128
FLOPS = 2 * 2 * T * 3 * E * D
BYTES = (
    T * D * 2 + 3 * E * D * 2 + 2 * C * 2 + T * 2 * E * 4 + 2 * T * 2 * H * 4
    + 3 * H * T * C * 2 + T * D * 4 + 3 * E * D * 4
)

F32 = mybir.dt.float32
BF16 = mybir.dt.bfloat16
I32 = mybir.dt.int32
U32 = mybir.dt.uint32
U8 = mybir.dt.uint8
E4 = mybir.dt.float8_e4m3fn_x4
E5 = mybir.dt.float8_e5m2_x4
ADD = mybir.AluOpType.add
SUB = mybir.AluOpType.subtract
MULT = mybir.AluOpType.mult
ACT = mybir.ActivationFunctionType


def tile_causalselfattention_pa_v_kernel(
    tc, x, w_attn, b_attn, q_ln_w, k_ln_w, qk, mean, rstd, grad_0, grad_1, grad_2, out_0, out_1
):
    nc = tc.nc
    with ExitStack() as ctx:
        keep = ctx.enter_context(tc.tile_pool(name="keep", bufs=1))
        load = ctx.enter_context(tc.tile_pool(name="load", bufs=2))
        work = ctx.enter_context(tc.tile_pool(name="work", bufs=2))
        psum = ctx.enter_context(tc.psum_pool(name="psum", bufs=8))
        ctx.enter_context(tc.manual_schedule())

        def load_g(grad, h0):
            t = load.tile([P, 4, 512], BF16, name="g_raw", bufs=4)
            nc.sync.dma_start(out=t[:], in_=grad[h0:h0 + 4].rearrange("h (p j) c -> p h (j c)", j=4))
            return t

        def load_u(n):
            t = load.tile([P, 4, 512], F32, name="u_raw", bufs=3)
            nc.sync.dma_start(out=t[:], in_=qk.rearrange("(p j) f -> p j f", j=4)[:, :, 512 * n:512 * n + 512])
            return t

        def load_v(h0):
            t = load.tile([P, 4, 512], BF16, name="g_raw", bufs=4)
            for h in range(4):
                nc.sync.dma_start(out=t[:, :, 128 * h:128 * h + 128], in_=grad_2[h0 + h].rearrange("(p j) c -> p j c", j=4))
            return t

        def load_w(src, parts=1):
            t = load.tile([P, 4, D], BF16, name="w_raw", bufs=3)
            rows = src.rearrange("(p j) d -> p j d", j=4)
            n = D // parts
            for k in range(parts):
                nc.sync.dma_start(out=t[:, :, n * k:n * k + n], in_=rows[:, :, n * k:n * k + n])
            return t

        def w_rows(g):
            return w_attn[512 * g:512 * g + 512, :]

        gains_row = keep.tile([P, 2 * C], BF16)
        nc.vector.memset(gains_row[:], 0.0)
        mu = keep.tile([P, 4, 16], F32)
        rs = keep.tile([P, 4, 16], F32)
        nc.sync.dma_start(out=gains_row[0:1, 0:C], in_=q_ln_w.unsqueeze(0))
        nc.sync.dma_start(out=gains_row[0:1, C:2 * C], in_=k_ln_w.unsqueeze(0))
        g_raw = {0: load_g(grad_0, 0)}
        nc.sync.dma_start(out=rs[:], in_=rstd.rearrange("(p j) n -> p j n", j=4))
        x_raw = load_w(x, 1)
        u_raw = {0: load_u(0)}
        nc.sync.dma_start(out=mu[:], in_=mean.rearrange("(p j) n -> p j n", j=4))
        w_raw = {4: load_w(w_rows(4))}
        v_raw = {4: load_v(0)}
        g_raw[1] = load_g(grad_0, 4)
        u_raw[1] = load_u(1)
        w_raw[0] = load_w(w_rows(0))
        v_raw[5] = load_v(4)

        tok = keep.tile([P, 4], F32)
        nc.gpsimd.iota(tok[:], pattern=[[1, 4]], base=0, channel_multiplier=4, allow_small_or_imprecise_dtypes=True)
        channel = keep.tile([P, 1], I32)
        nc.gpsimd.iota(channel[:], pattern=[[0, 1]], base=0, channel_multiplier=1)
        sign = keep.tile([P, 1], F32)
        odd = keep.tile([P, 1], I32)
        warm = keep.tile([P, 1], F32)
        nc.vector.memset(warm[:], 0.0)
        nc.scalar.activation(out=warm[:], in_=warm[:], func=ACT.Sin)
        ident = keep.tile([P, P], F32)
        make_identity(nc, ident[:])
        ident_b = keep.tile([P, P], BF16)
        nc.gpsimd.tensor_copy(out=ident_b[:], in_=ident[:])
        ones = keep.tile([P, P], BF16)
        nc.vector.memset(ones[:], 1.0)
        turns = work.tile([P, 2, 4, 64], F32, name="part", bufs=4)
        whole = work.tile([P, 2, 4, 64], I32, name="part", bufs=4)
        frac = work.tile([P, 2, 4, 64], F32, name="part", bufs=4)
        nc.vector.tensor_scalar(out=odd[:], in0=channel[:], scalar1=1, scalar2=None, op0=mybir.AluOpType.bitwise_and)
        nc.vector.tensor_scalar(out=turns[:, 0, :, 0:1], in0=tok[:].unsqueeze(2), scalar1=1.0 / (2.0 * math.pi), scalar2=None, op0=MULT)
        for n in (1, 4, 16):
            for k in (1, 2, 3):
                nc.vector.tensor_scalar(out=turns[:, 0, :, n * k:n * k + n], in0=turns[:, 0, :, 0:n],
                                        scalar1=10000.0 ** (-n * k / 64.0), scalar2=None, op0=MULT)
        nc.vector.tensor_scalar(out=sign[:], in0=odd[:], scalar1=-2.0, scalar2=1.0, op0=MULT, op1=ADD)
        for k in (1, 0):
            if k == 1:
                nc.vector.tensor_scalar(out=turns[:, 1], in0=turns[:, 0], scalar1=0.25, scalar2=None, op0=ADD)
            nc.vector.tensor_copy(out=whole[:, k], in_=turns[:, k])
        for k in (1, 0):
            nc.vector.tensor_tensor(out=frac[:, k], in0=turns[:, k], in1=whole[:, k], op=SUB)
        sines = work.tile([P, 4, 64, 2], F32, name="part", bufs=4)
        cosines = keep.tile([P, 4, 64], F32)
        nc.scalar.activation(out=cosines[:], in_=frac[:, 1], func=ACT.Sin, scale=2.0 * math.pi)
        nc.scalar.activation(out=sines[:], in_=frac[:, 0].unsqueeze(3).to_broadcast([P, 4, 64, 2]), func=ACT.Sin, scale=2.0 * math.pi)
        gains_bank = psum.tile([P, 2 * C], F32, name="bank")
        nc.tensor.matmul(gains_bank[:], lhsT=ones[:], rhs=gains_row[:], start=True, stop=True)
        gains = keep.tile([P, 2, C], F32)
        nc.scalar.copy(out=gains[:].rearrange("p w c -> p (w c)"), in_=gains_bank[:])
        column_bank = psum.tile([P, 2, 2], F32, name="bank")
        for w in range(2):
            nc.tensor.matmul(column_bank[:, w, :], lhsT=gains_row[:, C * w:C * w + C], rhs=ones[:, 0:2], start=True, stop=True)
        sines_bank = psum.tile([P, 4, P], F32, name="bank")
        for j in range(4):
            nc.tensor.transpose(sines_bank[:, j, :], sines[:, j].rearrange("p c e -> p (c e)"), ident[:])
        column = keep.tile([P, 2], F32)
        nc.vector.tensor_scalar(out=column[:], in0=column_bank[:, :, 0], scalar1=sign[:], scalar2=None, op0=MULT)
        sines_by_channel = []
        for w in range(2):
            t = keep.tile([P, 4, P], F32, name="sines_t%d" % w)
            nc.scalar.activation(out=t[:], in_=sines_bank[:], func=ACT.Copy, scale=column[:, w:w + 1])
            sines_by_channel.append(t)

        nmu = keep.tile([P, 4, 16], F32)
        r2 = keep.tile([P, 4, 16], F32)
        nc.gpsimd.tensor_tensor(out=r2[:], in0=rs[:], in1=rs[:], op=MULT)
        nc.gpsimd.tensor_scalar(out=r2[:], in0=r2[:], scalar1=-1.0 / C, scalar2=0.0, op0=MULT, op1=ADD)

        ct = keep.tile([P, 2, 4, 64, 2], F32)
        st = {}

        def cos_table(w, source):
            nc.vector.tensor_tensor(out=ct[:, w], in0=cosines[:].unsqueeze(3).to_broadcast([P, 4, 64, 2]),
                                    in1=source.rearrange("p (c e) -> p c e", e=2).unsqueeze(1).to_broadcast([P, 4, 64, 2]), op=MULT)

        def sin_table(w):
            bank = psum.tile([P, 4, P], F32, name="bank")
            for j in range(4):
                nc.tensor.transpose(bank[:, j, :], sines_by_channel[w][:, j, :], ident[:])
            st[w] = bank

        x_codes = keep.tile([P, D], U32, align_bytes=64)
        x_scales = keep.tile([P, D], U8, align_bytes=64)
        w_codes = keep.tile([P, 6, D], U32, align_bytes=64)
        w_scales = keep.tile([P, 6, D], U8, align_bytes=64)
        t_codes = keep.tile([P, 6, 512], U32, align_bytes=64)
        t_scales = keep.tile([P, 6, 512], U8, align_bytes=64)

        def copy(eng, dst, src):
            if eng == "s":
                nc.scalar.copy(out=dst, in_=src)
            else:
                nc.vector.tensor_copy(out=dst, in_=src)

        def interleave(eng, dst, src):
            copy(eng, dst.rearrange("p (c i) t -> p c t i", i=4), src.rearrange("p t (c i) -> p c t i", i=4))

        def quant(codes, scales, src, fmt):
            nc.vector.quantize_mx(out=codes.bitcast(fmt), scales=scales, in_=src.rearrange("p n t -> p (n t)"))

        groups = {}

        def new_group(g):
            dz = work.tile([P, 512, 4], BF16, name="dz", align_bytes=64, bufs=2)
            codes = work.tile([P, 512], U32, name="dzc", align_bytes=64, bufs=4)
            scales = work.tile([P, 512], U8, name="dzs", align_bytes=64, bufs=4)
            groups[g] = (dz, codes, scales)

        ready = []

        def mul_head(g, h):
            codes, scales = groups[g][1], groups[g][2]
            f = slice(128 * h, 128 * h + 128)
            banks = []
            for dh in range(2):
                ps = psum.tile([P, 512], F32, name="bank")
                d = slice(512 * dh, 512 * dh + 512)
                nc.tensor.matmul_mx(out=ps[:], lhsT=codes[:, f].bitcast(E5), lhsT_scale=scales[:, f],
                                    rhs=x_codes[:, d].bitcast(E4), rhs_scale=x_scales[:, d], start=True, stop=True)
                banks.append(ps)
            ready.append((512 * g + 128 * h, banks))

        def drain_head(engs):
            row0, banks = ready.pop(0)
            o = work.tile([P, D], F32, name="o1", bufs=5)
            for dh in range(2):
                copy(engs[dh], o[:, 512 * dh:512 * dh + 512], banks[dh][:])
            nc.sync.dma_start(out=out_1[row0:row0 + 128, :], in_=o[:])

        turned = {}

        def turn(g):
            words = groups[g][0][:].rearrange("p f t -> p (f t)").bitcast(F32)
            banks = []
            for u in range(2):
                tp = psum.tile([P, 4, P], F32, name="bank")
                for t in range(4):
                    nc.tensor.transpose(tp[:, t, :], words[:, 2 * t + u:1024:8], ident[:])
                banks.append(tp)
            turned[g] = banks

        def turn_v(g):
            banks = []
            for b in range(2):
                tp = psum.tile([P, 2, 2, P], F32, name="bank")
                for k in range(2):
                    words = v_raw[g][:, 2 * b + k, :].bitcast(F32)
                    for u in range(2):
                        nc.tensor.transpose(tp[:, k, u, :], words[:, u:256:2], ident[:])
                banks.append(tp)
            turned[g] = banks

        def untangle_v(g, engs):
            dzt = work.tile([P, 512, 4], BF16, name="dzt", align_bytes=64, bufs=2)
            words = dzt[:].rearrange("m n t -> m (n t)").bitcast(F32).rearrange("m (p b k) -> m b p k", b=2, k=4)
            for b in range(2):
                copy(engs[b], words[:, b], turned[g][b][:].rearrange("m k u p -> m p (k u)"))
            turned[g] = dzt

        def untangle(g, engs):
            if g >= 4:
                untangle_v(g, engs)
                return
            dzt = work.tile([P, 512, 4], BF16, name="dzt", align_bytes=64, bufs=2)
            for u in range(2):
                copy(engs[u], dzt[:].rearrange("m (p u e) t -> m u p e t", u=2, e=2)[:, u],
                     turned[g][u][:].rearrange("m t p -> m (t p)").bitcast(BF16).rearrange("m (t p e) -> m p e t", t=4, e=2))
            turned[g] = dzt

        def quant_turned(g):
            quant(t_codes[:, g, :], t_scales[:, g, :], turned[g][:], E5)

        w_order = [4, 0, 5, 1, 2, 3]
        moved = {}
        w_int = {}
        w_wait = []

        def w_move(k):
            g, q = w_order[k // 4], k % 4
            bank = psum.tile([P, 256, 4], BF16, name="bank")
            for t in (0, 2):
                nc.tensor.matmul(bank[:, :, t:t + 2], lhsT=ident_b[:],
                                 rhs=w_raw[g][:, t:t + 2, 256 * q:256 * q + 256].rearrange("p t c -> p c t"), start=True, stop=True)
            moved[k] = bank[:]

        def w_spread(k):
            eng = "v" if k in by_vector else "s"
            g, q = w_order[k // 4], k % 4
            if q % 2 == 0:
                half = work.tile([P, 512, 4], BF16, name="w_int", align_bytes=64, bufs=4)
                w_int[k // 2] = half
            dst = w_int[k // 2][:, 256 * (q % 2):256 * (q % 2) + 256, :]
            if k in moved:
                copy(eng, dst, moved[k])
            else:
                interleave(eng, dst, w_raw[g][:, :, 256 * q:256 * q + 256])
            if q % 2 == 1:
                w_wait.append(k // 2)

        def w_quant():
            if w_wait:
                m = w_wait.pop(0)
                g, n0 = w_order[m // 2], 512 * (m % 2)
                quant(w_codes[:, g, n0:n0 + 512], w_scales[:, g, n0:n0 + 512], w_int[m][:], E4)

        units = [(2 * n, 2) for n in range(7)] + [(14, 1), (15, 1)]
        state = [{} for n in range(len(units))]
        q1_by_scalar = ()

        def table(n, cols):
            return ct[:, units[n][0] // 8].rearrange("p j c e -> p (j c e)")[:, cols]

        def by_gpsimd(n):
            return 384 if 1 <= n <= 6 else 0

        def st_ag(n):
            i, m = units[n]
            a1 = work.tile([P, 512], F32, name="a1", bufs=1)
            g = by_gpsimd(n)
            if g:
                nc.gpsimd.tensor_tensor(out=a1[:, 0:g], in0=g_raw[i // 4][:, i % 4 + 1, 0:g], in1=table(n, slice(0, g)), op=MULT)
            state[n]["a1"] = a1

        def st_a(n):
            i, m = units[n]
            a0 = work.tile([P, 512], F32, name="a0", bufs=2)
            nc.vector.tensor_tensor(out=a0[:], in0=g_raw[i // 4][:, i % 4, :], in1=table(n, slice(0, 512)), op=MULT)
            g = by_gpsimd(n)
            if m == 2 and g < 512:
                nc.vector.tensor_tensor(out=state[n]["a1"][:, g:512], in0=g_raw[i // 4][:, i % 4 + 1, g:512], in1=table(n, slice(g, 512)), op=MULT)
            state[n]["a0"] = a0

        def st_b(n):
            i, m = units[n]
            b = work.tile([P, 2, 512], F32, name="b", bufs=2)
            for k in range(m):
                for j in range(4):
                    w = slice(128 * j, 128 * j + 128)
                    nc.vector.scalar_tensor_tensor(
                        out=b[:, k, w].rearrange("p (c e) -> p c e", e=2),
                        in0=g_raw[i // 4][:, i % 4 + k, w].rearrange("p (c e) -> p c e", e=2)[:, :, ::-1],
                        scalar=rs[:, j, i + k:i + k + 1], in1=st[i // 8][:, j, :].rearrange("p (c e) -> p c e", e=2), op0=MULT, op1=MULT)
            state[n]["b"] = b

        def st_c(n):
            i, m = units[n]
            a, b = (state[n]["a0"], state[n]["a1"]), state[n]["b"]
            c = work.tile([P, 2, 512], F32, name="c", bufs=2)
            q1 = work.tile([P, 2, 4], F32, name="q1", bufs=2)
            for k in range(m):
                for j in range(4):
                    w = slice(128 * j, 128 * j + 128)
                    nc.vector.scalar_tensor_tensor(
                        out=c[:, k, w], in0=a[k][:, w], scalar=rs[:, j, i + k:i + k + 1], in1=b[:, k, w], op0=MULT, op1=ADD,
                        accum_out=None if n in q1_by_scalar else q1[:, k, j:j + 1])
                    if n in q1_by_scalar:
                        nc.scalar.activation(out=b[:, k, w], in_=c[:, k, w], func=ACT.Identity, accum_out=q1[:, k, j:j + 1])
            state[n]["c"], state[n]["q1"] = c, q1

        def st_q(n):
            i, m = units[n]
            a, c = (state[n]["a0"], state[n]["a1"]), state[n]["c"]
            q2 = work.tile([P, 2, 4], F32, name="q2", bufs=2)
            rows = [(0, j) for j in range(4)]
            if m == 2:
                rows = rows[0:3] + [(1, j) for j in range(4)] + rows[3:]
            for k, j in rows:
                    w = slice(128 * j, 128 * j + 128)
                    h = i % 4 + k
                    nc.vector.scalar_tensor_tensor(
                        out=a[k][:, w], in0=u_raw[i // 4][:, j, 128 * h:128 * h + 128], scalar=nmu[:, j, i + k:i + k + 1], in1=c[:, k, w],
                        op0=ADD, op1=MULT, accum_out=q2[:, k, j:j + 1])
            state[n]["q2"] = q2

        def per_head(t, n):
            i, m = units[n]
            return t[:, :, i:i + m].rearrange("p j n -> p n j")

        def st_k2(n):
            i, m = units[n]
            k2 = work.tile([P, 2, 4], F32, name="k2", bufs=2)
            nc.vector.tensor_tensor(out=k2[:, 0:m], in0=state[n]["q2"][:, 0:m], in1=per_head(r2, n), op=MULT)
            state[n]["k2"] = k2

        def st_km(n):
            i, m = units[n]
            km = work.tile([P, 2, 4], F32, name="km", bufs=2)
            nc.vector.tensor_tensor(out=km[:, 0:m], in0=state[n]["k2"][:, 0:m], in1=per_head(nmu, n), op=MULT)
            state[n]["km"] = km

        def st_k1(n):
            i, m = units[n]
            k1 = work.tile([P, 2, 4], F32, name="k1", bufs=2)
            nc.vector.scalar_tensor_tensor(out=k1[:, 0:m], in0=state[n]["q1"][:, 0:m], scalar=-1.0 / C, in1=state[n]["km"][:, 0:m], op0=MULT, op1=ADD)
            state[n]["k1"] = k1

        def st_t(n):
            i, m = units[n]
            t1 = work.tile([P, 2, 512], F32, name="t1", bufs=2)
            for k in range(m):
                h = i % 4 + k
                for j in range(4):
                    o, u = t1[:, k, 128 * j:128 * j + 128], u_raw[i // 4][:, j, 128 * h:128 * h + 128]
                    k2, k1 = state[n]["k2"][:, k, j:j + 1], state[n]["k1"][:, k, j:j + 1]
                    if n >= 6 and 4 * k + j >= (4, 0, 1)[n - 6]:
                        nc.vector.tensor_scalar(out=o, in0=u, scalar1=k2, scalar2=k1, op0=MULT, op1=ADD)
                    else:
                        nc.scalar.activation(out=o, in_=u, func=ACT.Identity, scale=k2, bias=k1)
            state[n]["t1"] = t1

        def st_f(n):
            i, m = units[n]
            if i % 4 == 0:
                new_group(i // 4)
            dz = groups[i // 4][0]
            for k in range(m):
                h = i % 4 + k
                nc.vector.tensor_tensor(out=dz[:, 128 * h:128 * h + 128, :].rearrange("p (c i) t -> p c t i", i=4),
                                        in0=state[n]["c"][:, k].rearrange("p (t c i) -> p c t i", t=4, i=4),
                                        in1=state[n]["t1"][:, k].rearrange("p (t c i) -> p c t i", t=4, i=4), op=ADD)

        def st_z(n):
            i, m = units[n]
            g = i // 4
            dz, codes, scales = groups[g]
            f = slice(128 * (i % 4), 128 * (i % 4 + m))
            quant(codes[:, f], scales[:, f], dz[:, f, :], E5)
            for k in range(m):
                mul_head(g, i % 4 + k)

        def out0_passes(ps, tb, dh, order, first, final):
            t = slice(128 * tb, 128 * tb + 128)
            d = slice(512 * dh, 512 * dh + 512)
            for k, g in enumerate(order):
                nc.tensor.matmul_mx(out=ps[:], lhsT=t_codes[:, g, t].bitcast(E5), lhsT_scale=t_scales[:, g, t],
                                    rhs=w_codes[:, g, d].bitcast(E4), rhs_scale=w_scales[:, g, d],
                                    start=first and k == 0, stop=final and k == len(order) - 1)

        def v_interleave(g, h, eng):
            interleave(eng, groups[g][0][:, 128 * h:128 * h + 128, :], v_raw[g][:, :, 128 * h:128 * h + 128])

        direct = (0, 1, 2, 4, 8, 12)
        by_vector = (1,)
        cos_table(0, gains_bank[:, 0:C])
        x_int = []
        for q in range(4):
            if q % 2 == 0:
                half = work.tile([P, 512, 4], BF16, name="w_int", align_bytes=64, bufs=4)
                x_int.append(half)
            interleave("s", x_int[q // 2][:, 256 * (q % 2):256 * (q % 2) + 256, :], x_raw[:, :, 256 * q:256 * q + 256])
        sin_table(0)
        st_ag(0)
        st_a(0)
        st_b(0)
        st_c(0)
        nc.vector.tensor_scalar(out=nmu[:], in0=mu[:], scalar1=-1.0, scalar2=None, op0=MULT)
        new_group(4)
        for k in range(1):
            w_spread(k)
        for h in range(4):
            v_interleave(4, h, "s")
        st_q(0)
        st_ag(1)
        st_b(1)
        st_k2(0)
        for q in range(2):
            d = slice(512 * q, 512 * q + 512)
            quant(x_codes[:, d], x_scales[:, d], x_int[q][:], E4)
            if q == 0:
                st_km(0)
        st_k1(0)
        turn_v(4)
        st_a(1)
        st_t(0)

        next_w = len(range(1))
        pieces = [0, 3, 4, 4, 4, 4, 2, 2, 0]
        to_untangle = [4]
        to_quant = []
        parked = {}
        opened = {}

        def open_bank(tb, dh):
            ps = psum.tile([P, 512], F32, name="bank")
            out0_passes(ps, tb, dh, w_order[0:5], True, False)
            opened[(tb, dh)] = ps

        def park_bank(tb, dh):
            ps = psum.tile([P, 512], F32, name="bank")
            out0_passes(ps, tb, dh, w_order[0:4], True, True)
            part = work.tile([P, 512], F32, name="part", bufs=4)
            nc.scalar.copy(out=part[:], in_=ps[:])
            parked[(tb, dh)] = part

        for n in range(1, 9):
            todo = list(range(next_w, next_w + pieces[n]))
            next_w += pieces[n]
            if n == 1:
                w_raw[5] = load_w(w_rows(5))
                g_raw[2] = load_g(grad_1, 0)
            if n == 2:
                u_raw[2] = load_u(2)
            if n == 3:
                w_raw[1] = load_w(w_rows(1))
                g_raw[3] = load_g(grad_1, 4)
            if n == 4:
                u_raw[3] = load_u(3)
                w_raw[2] = load_w(w_rows(2))
            if n == 5:
                w_raw[3] = load_w(w_rows(3))
            if to_untangle:
                g = to_untangle.pop(0)
                untangle(g, "ss")
                to_quant.append(g)
            while ready:
                drain_head("ss")
            for k in todo[0:2]:
                if k not in direct:
                    w_move(k)
            for k in todo[0:2]:
                w_spread(k)
            if n == 1:
                quant(groups[4][1][:], groups[4][2][:], groups[4][0][:], E5)
                for h in range(3):
                    mul_head(4, h)
            if n == 2:
                mul_head(4, 3)
            if n == 3:
                quant(groups[5][1][:], groups[5][2][:], groups[5][0][:], E5)
                turn_v(5)
                to_untangle.append(5)
            for h in {3: (0,), 4: (1,), 5: (2,), 6: (3,)}.get(n, ()):
                mul_head(5, h)
            if n == 6:
                park_bank(2, 0)
                park_bank(2, 1)
            if n == 8:
                open_bank(1, 0)
            st_c(n)
            while ready:
                drain_head("ss")
            for k in todo[2:]:
                if k not in direct:
                    w_move(k)
                    w_spread(k)
            for k in todo[2:]:
                if k in direct:
                    w_spread(k)
            if n == 6:
                park_bank(3, 0)
                park_bank(3, 1)
            st_f(n - 1)
            st_q(n)
            if n < 8:
                st_ag(n + 1)
                st_b(n + 1)
            st_z(n - 1)
            i, m = units[n - 1]
            if (i + m) % 4 == 0:
                turn((i + m) // 4 - 1)
                to_untangle.append((i + m) // 4 - 1)
            if n in (1, 2):
                if n == 1:
                    new_group(5)
                for h in (2 * n - 2, 2 * n - 1):
                    v_interleave(5, h, "s")
            st_k2(n)
            if to_quant:
                quant_turned(to_quant.pop(0))
            if n == 7:
                open_bank(0, 0)
            if n in range(1, 7):
                w_quant()
            st_km(n)
            if n == 8:
                w_quant()
                w_quant()
            if n < 8:
                st_a(n + 1)
            st_k1(n)
            if n == 2:
                cos_table(1, gains[:, 1])
                sin_table(1)
            if n in range(2, 6):
                w_quant()
            st_t(n)
            if n == 7:
                open_bank(0, 1)
            if n == 8:
                open_bank(1, 1)

        while ready:
            drain_head("ss")
        for h in ():
            mul_head(5, h)
        while w_wait:
            w_quant()
        st_f(8)
        turn(3)
        st_z(8)
        for h in ():
            drain_head("sv")
        untangle(3, "sv")
        quant_turned(3)
        while ready:
            drain_head("sv")
        for k, tb in enumerate((0, 2, 1, 3)):
            o = work.tile([P, D], F32, name="o1", bufs=5)
            for dh in range(2):
                d = slice(512 * dh, 512 * dh + 512)
                if tb < 2:
                    ps = opened[(tb, dh)]
                    out0_passes(ps, tb, dh, [3], False, True)
                    nc.scalar.copy(out=o[:, d], in_=ps[:])
                else:
                    ps = psum.tile([P, 512], F32, name="bank")
                    out0_passes(ps, tb, dh, [2, 3], True, True)
                    nc.vector.tensor_tensor(out=o[:, d], in0=ps[:], in1=parked[(tb, dh)][:], op=ADD)
                nc.sync.dma_start(out=out_0[128 * tb:128 * tb + 128, d], in_=o[:, d])
